import numpy as np
import ml_dtypes


def mxq(x, axis, fmt="e4m3"):
    dtype, down = {"e4m3": (ml_dtypes.float8_e4m3fn, 7), "e5m2": (ml_dtypes.float8_e5m2, 14)}[fmt]
    v = np.moveaxis(np.asarray(x, np.float32).astype(ml_dtypes.bfloat16).astype(np.float64), axis, -1)
    blocks = v.reshape(v.shape[:-1] + (-1, 32))
    amax = np.abs(blocks).max(-1, keepdims=True)
    byte = np.maximum(np.where(amax > 0, np.frexp(amax)[1] - 1 + 127, 0) - down, 1)
    scale = np.exp2(byte - 127.0)
    codes = (blocks / scale).astype(np.float32).astype(dtype).astype(np.float64)
    return np.moveaxis((codes * scale).reshape(v.shape), -1, axis)


WIDE = False


def mx_kscale(k):
    if not WIDE:
        return np.ones(k)
    levels = np.array([10, -10, 5, -5, 0])
    a = np.random.permutation(np.resize(levels, k // 512 * 4)).reshape(k // 512, 4)
    idx = np.arange(k)
    return np.exp2(a[idx // 512, idx % 128 // 32])


BF16 = ml_dtypes.bfloat16


def bf(x):
    return np.asarray(x, np.float32).astype(BF16)


def f64(x):
    return np.asarray(x).astype(np.float64)


B, CI, CO, N, KM, M = 2, 512, 128, 1024, 32, 512
R = 6.0
A = np.sqrt(R) / N ** 0.25


def setup_inputs():
    u = mx_kscale(CI * KM)[::KM]
    t = mx_kscale(M)
    return {
        "x": bf((np.random.standard_normal((B, CI, N)) + A) * u[None, :, None]),
        "wbases": bf((np.random.standard_normal((B, N, M)) + A) / (R * np.sqrt(N))),
        "bases": bf(np.random.standard_normal((B, N, M)) / np.sqrt(M) / t),
        "weights": bf(np.random.standard_normal((CI, CO, KM)) / np.sqrt(CI * KM) / u[:, None, None]),
        "D": bf(np.random.standard_normal((KM, M)) * t),
    }


def reference(x, wbases, bases, weights, D):
    x_hat = f64(x) @ f64(wbases)[:, :, :M]
    z = (x_hat[:, :, None, :] * f64(D)[None, None, :, :]).reshape(B, CI * KM, M)
    w2 = f64(weights).transpose(0, 2, 1).reshape(CI * KM, CO)
    y_hat = mxq(w2, 0, "e4m3").T @ mxq(z, 1, "e4m3")
    return mxq(y_hat, 2, "e4m3") @ mxq(f64(bases)[:, :, :M], 2, "e4m3").transpose(0, 2, 1)

@@ -1,0 +1,259 @@
+from contextlib import ExitStack
+
+import concourse.mybir as mybir
+from concourse.masks import make_identity
+
+BF16 = mybir.dt.bfloat16
+F32 = mybir.dt.float32
+U32 = mybir.dt.uint32
+U8 = mybir.dt.uint8
+FP8X4 = mybir.dt.float8_e4m3fn_x4
+MULT = mybir.AluOpType.mult
+
+B, CI, CO, N, KM, M = 2, 512, 128, 1024, 32, 512
+
+P = 128
+PACK = 4
+K_PASS = P * PACK
+CH_PASS = K_PASS // KM
+REP = P // CH_PASS
+PASSES = CI // CH_PASS
+CH_TILES = CI // P
+TILE_PASSES = P // CH_PASS
+N_CHUNKS = N // P
+M_CHUNKS = M // P
+W_PASSES = 4
+W_CH = W_PASSES * CH_PASS
+W_LOADS = PASSES // W_PASSES
+W_BUFS = 4
+N_HALF = 512
+
+FLOPS = 2 * B * (CI * N * M + CI * KM * CO * M + CO * M * N)
+
+
+def tile_phydgalerkinconv_k_kernel(tc, x, wbases, bases, weights, D, out):
+    nc = tc.nc
+    with ExitStack() as ctx:
+        const = ctx.enter_context(tc.tile_pool(name="const", bufs=1))
+        inputs = ctx.enter_context(tc.tile_pool(name="inputs", bufs=1))
+        w_in = ctx.enter_context(tc.tile_pool(name="w_in", bufs=W_BUFS))
+        keep = ctx.enter_context(tc.tile_pool(name="keep", bufs=1))
+        work = ctx.enter_context(tc.tile_pool(name="work", bufs=2))
+        z_pool = ctx.enter_context(tc.tile_pool(name="z_pool", bufs=4))
+        acc_psum = ctx.enter_context(tc.psum_pool(name="acc_psum", bufs=2))
+        rep_psum = ctx.enter_context(tc.psum_pool(name="rep_psum", bufs=3))
+        xh_psum = ctx.enter_context(tc.psum_pool(name="xh_psum", bufs=1))
+        tr_psum = ctx.enter_context(tc.psum_pool(name="tr_psum", bufs=2))
+
+        x_sb = [inputs.tile([P, CH_TILES, N], BF16, name="x_sb%d" % b) for b in range(B)]
+        wb_sb = [inputs.tile([P, N_CHUNKS, M], BF16, name="wb_sb%d" % b) for b in range(B)]
+        bases_sb = [inputs.tile([P, N_CHUNKS, M], BF16, name="bases_sb%d" % b) for b in range(B)]
+        w_sb = []
+
+        def load_x(b, it):
+            nc.sync.dma_start(out=x_sb[b][:, it, :], in_=x[b, it * P : (it + 1) * P, :])
+
+        def load_weights(h):
+            w_tile = w_in.tile([P, W_CH, KM], BF16, name="w_tile")
+            nc.sync.dma_start(
+                out=w_tile[:],
+                in_=weights[h * W_CH : (h + 1) * W_CH, :, :].rearrange("i o j -> o i j"),
+            )
+            w_sb.append(w_tile)
+
+        d_rows = const.tile([P, PACK, M], BF16)
+
+        def load_the_rest():
+            nc.sync.dma_start(out=wb_sb[1][:], in_=wbases[1].rearrange("(c p) k -> p c k", p=P))
+            for it in range(CH_TILES):
+                load_x(1, it)
+            for b in range(B):
+                nc.sync.dma_start(
+                    out=bases_sb[b][:], in_=bases[b].rearrange("(c p) k -> p c k", p=P)
+                )
+
+        load_x(0, 0)
+        nc.sync.dma_start(out=wb_sb[0][:], in_=wbases[0].rearrange("(c p) k -> p c k", p=P))
+        for q in range(CH_PASS):
+            nc.sync.dma_start(
+                out=d_rows[q * REP : (q + 1) * REP, :, :],
+                in_=D.rearrange("(h t) k -> h t k", t=PACK),
+            )
+        load_weights(0)
+        load_weights(1)
+        load_x(0, 1)
+        load_weights(2)
+        load_weights(3)
+        load_x(0, 2)
+        load_x(0, 3)
+
+        ident_bf = const.tile([P, P], BF16)
+        make_identity(nc, ident_bf[:])
+        ident_f32 = const.tile([P, P], F32)
+        make_identity(nc, ident_f32[:])
+
+        d_grouped = const.tile([P, M, PACK], BF16)
+        nc.vector.tensor_copy(out=d_grouped[:], in_=d_rows[:].rearrange("p t k -> p k t"))
+
+        w_codes = keep.tile([P, PASSES, CO], U32, align_bytes=64)
+        w_scales = keep.tile([P, PASSES, CO], U8, align_bytes=64)
+        b_codes = [keep.tile([P, N], U32, align_bytes=64, name="b_codes%d" % b) for b in range(B)]
+        b_scales = [keep.tile([P, N], U8, align_bytes=64, name="b_scales%d" % b) for b in range(B)]
+
+        def quantise_weights(h):
+            words = (
+                w_sb[h][:]
+                .rearrange("o i j -> o (i j)")
+                .bitcast(F32)
+                .rearrange("o (g p u) -> o g p u", g=W_PASSES, p=P, u=2)
+            )
+            w_grouped = work.tile([P, W_PASSES, CO, PACK], BF16, align_bytes=64)
+            for half in range(W_PASSES // 2):
+                wT_ps = tr_psum.tile([P, 2, 2, CO], F32, tag="tr")
+                for gg in range(2):
+                    for u in range(2):
+                        nc.tensor.transpose(
+                            wT_ps[:, gg, u, :], words[:, 2 * half + gg, :, u], ident_f32[:]
+                        )
+                nc.scalar.copy(
+                    out=w_grouped[:, 2 * half : 2 * half + 2, :, :].bitcast(F32),
+                    in_=wT_ps[:].rearrange("p g u o -> p g o u"),
+                )
+            passes = slice(h * W_PASSES, (h + 1) * W_PASSES)
+            nc.vector.quantize_mx(
+                out=w_codes[:, passes, :].rearrange("p g o -> p (g o)").bitcast(FP8X4),
+                scales=w_scales[:, passes, :].rearrange("p g o -> p (g o)"),
+                in_=w_grouped[:].rearrange("p g o t -> p (g o t)"),
+            )
+
+        def quantise_bases(b):
+            words = bases_sb[b][:].bitcast(F32)
+            b_grouped = work.tile([P, N_CHUNKS, P, PACK], BF16, align_bytes=64)
+            for pair in range(N_CHUNKS // 2):
+                bT_ps = tr_psum.tile([P, 2, 2, P], F32, tag="tr")
+                for cc in range(2):
+                    for u in range(2):
+                        nc.tensor.transpose(
+                            bT_ps[:, cc, u, :],
+                            words[:, 2 * pair + cc, u * P : (u + 1) * P],
+                            ident_f32[:],
+                        )
+                nc.scalar.copy(
+                    out=b_grouped[:, 2 * pair : 2 * pair + 2, :, :].bitcast(F32),
+                    in_=bT_ps[:].rearrange("p c u n -> p c n u"),
+                )
+            nc.vector.quantize_mx(
+                out=b_codes[b][:].bitcast(FP8X4),
+                scales=b_scales[b][:],
+                in_=b_grouped[:].rearrange("p c n t -> p (c n t)"),
+            )
+
+        def project_channels(b, it):
+            xT_ps = tr_psum.tile([P, N_CHUNKS, P], BF16, tag="tr")
+            for c in range(N_CHUNKS):
+                nc.tensor.transpose(xT_ps[:, c, :], x_sb[b][:, it, c * P : (c + 1) * P], ident_bf[:])
+            xT_sb = work.tile([P, N_CHUNKS, P], BF16)
+            nc.scalar.copy(out=xT_sb[:], in_=xT_ps[:])
+            xh_ps = xh_psum.tile([P, M_CHUNKS, P], F32)
+            for kc in range(M_CHUNKS):
+                for c in range(N_CHUNKS):
+                    nc.tensor.matmul(
+                        xh_ps[:, kc, :],
+                        lhsT=wb_sb[b][:, c, kc * P : (kc + 1) * P],
+                        rhs=xT_sb[:, c, :],
+                        start=(c == 0),
+                        stop=(c == N_CHUNKS - 1),
+                    )
+            x_rep = work.tile([P, TILE_PASSES, M_CHUNKS, CH_PASS, REP], F32)
+            for gl in range(TILE_PASSES):
+                nc.scalar.copy(
+                    out=x_rep[:, gl, :, :, :],
+                    in_=xh_ps[:, :, gl * CH_PASS : (gl + 1) * CH_PASS]
+                    .unsqueeze(3)
+                    .to_broadcast([P, M_CHUNKS, CH_PASS, REP]),
+                )
+            return x_rep
+
+        def contract_pass(b, g, x_rep, acc):
+            gl = g % TILE_PASSES
+            x_wide = rep_psum.tile([P, M], F32)
+            for kc in range(M_CHUNKS):
+                nc.tensor.transpose(
+                    x_wide[:, kc * P : (kc + 1) * P],
+                    x_rep[:, gl, kc, :, :].rearrange("p i r -> p (i r)"),
+                    ident_f32[:],
+                )
+            z_bf = z_pool.tile([P, M, PACK], BF16, align_bytes=64)
+            nc.vector.tensor_tensor(
+                out=z_bf[:],
+                in0=x_wide[:].unsqueeze(2).to_broadcast([P, M, PACK]),
+                in1=d_grouped[:],
+                op=MULT,
+            )
+            z_codes = z_pool.tile([P, M], U32, align_bytes=64)
+            z_scales = z_pool.tile([P, M], U8, align_bytes=64)
+            nc.vector.quantize_mx(
+                out=z_codes[:].bitcast(FP8X4),
+                scales=z_scales[:],
+                in_=z_bf[:].rearrange("p k t -> p (k t)"),
+            )
+            nc.tensor.matmul_mx(
+                out=acc[:],
+                lhsT=w_codes[:, g, :].bitcast(FP8X4),
+                lhsT_scale=w_scales[:, g, :],
+                rhs=z_codes[:].bitcast(FP8X4),
+                rhs_scale=z_scales[:],
+                start=(g == 0),
+                stop=(g == PASSES - 1),
+            )
+
+        def reconstruct(b, acc):
+            y_sb = work.tile([P, M], F32)
+            nc.scalar.copy(out=y_sb[:], in_=acc[:])
+            y_cols = y_sb[:].rearrange("o (u p e) -> o u e p", u=2, p=P, e=2)
+            yT_ps = tr_psum.tile([P, PACK, CO], F32, tag="tr")
+            for u in range(2):
+                for e in range(2):
+                    nc.tensor.transpose(yT_ps[:, 2 * u + e, :], y_cols[:, u, e, :], ident_f32[:])
+            y_grouped = work.tile([P, CO, PACK], BF16, align_bytes=64)
+            nc.scalar.copy(out=y_grouped[:], in_=yT_ps[:].rearrange("p t o -> p o t"))
+            y_codes = work.tile([P, CO], U32, align_bytes=64)
+            y_scales = work.tile([P, CO], U8, align_bytes=64)
+            nc.vector.quantize_mx(
+                out=y_codes[:].bitcast(FP8X4),
+                scales=y_scales[:],
+                in_=y_grouped[:].rearrange("p o t -> p (o t)"),
+            )
+            for half in range(N // N_HALF):
+                cols = slice(half * N_HALF, (half + 1) * N_HALF)
+                o_ps = tr_psum.tile([P, N_HALF], F32, tag="tr")
+                nc.tensor.matmul_mx(
+                    out=o_ps[:],
+                    lhsT=y_codes[:].bitcast(FP8X4),
+                    lhsT_scale=y_scales[:],
+                    rhs=b_codes[b][:, cols].bitcast(FP8X4),
+                    rhs_scale=b_scales[b][:, cols],
+                    start=True,
+                    stop=True,
+                )
+                o_sb = work.tile([P, N_HALF], F32)
+                nc.scalar.copy(out=o_sb[:], in_=o_ps[:])
+                nc.sync.dma_start(out=out[b, :, cols], in_=o_sb[:])
+
+        for b in range(B):
+            acc = acc_psum.tile([P, M], F32)
+            for it in range(CH_TILES):
+                x_rep = project_channels(b, it)
+                for gl in range(TILE_PASSES):
+                    g = it * TILE_PASSES + gl
+                    if b == 0 and g % W_PASSES == 0:
+                        h = g // W_PASSES
+                        quantise_weights(h)
+                        if h + W_BUFS < W_LOADS:
+                            load_weights(h + W_BUFS)
+                        if h + W_BUFS == W_LOADS - 1:
+                            load_the_rest()
+                    contract_pass(b, g, x_rep, acc)
+                if it == CH_TILES - 2:
+                    quantise_bases(b)
+            reconstruct(b, acc)

@@ -18,6 +18,7 @@ K_PASS = P * PACK
 CH_PASS = K_PASS // KM
 REP = P // CH_PASS
 PASSES = CI // CH_PASS
+ALL_PASSES = B * PASSES
 CH_TILES = CI // P
 TILE_PASSES = P // CH_PASS
 N_CHUNKS = N // P
@@ -27,6 +28,7 @@ W_CH = W_PASSES * CH_PASS
 W_LOADS = PASSES // W_PASSES
 W_BUFS = 4
 N_HALF = 512
+ROUND = 3
 
 FLOPS = 2 * B * (CI * N * M + CI * KM * CO * M + CO * M * N)
 
@@ -34,14 +36,16 @@ FLOPS = 2 * B * (CI * N * M + CI * KM * CO * M + CO * M * N)
 def tile_phydgalerkinconv_k_kernel(tc, x, wbases, bases, weights, D, out):
     nc = tc.nc
     with ExitStack() as ctx:
+        ctx.enter_context(tc.manual_schedule())
         const = ctx.enter_context(tc.tile_pool(name="const", bufs=1))
         inputs = ctx.enter_context(tc.tile_pool(name="inputs", bufs=1))
         w_in = ctx.enter_context(tc.tile_pool(name="w_in", bufs=W_BUFS))
         keep = ctx.enter_context(tc.tile_pool(name="keep", bufs=1))
         work = ctx.enter_context(tc.tile_pool(name="work", bufs=2))
-        z_pool = ctx.enter_context(tc.tile_pool(name="z_pool", bufs=4))
-        acc_psum = ctx.enter_context(tc.psum_pool(name="acc_psum", bufs=2))
-        rep_psum = ctx.enter_context(tc.psum_pool(name="rep_psum", bufs=3))
+        wide_pool = ctx.enter_context(tc.tile_pool(name="wide_pool", bufs=ROUND))
+        z_pool = ctx.enter_context(tc.tile_pool(name="z_pool", bufs=2 * ROUND))
+        acc_psum = ctx.enter_context(tc.psum_pool(name="acc_psum", bufs=1))
+        wide_psum = ctx.enter_context(tc.psum_pool(name="wide_psum", bufs=ROUND))
         xh_psum = ctx.enter_context(tc.psum_pool(name="xh_psum", bufs=1))
         tr_psum = ctx.enter_context(tc.psum_pool(name="tr_psum", bufs=2))
 
@@ -53,6 +57,9 @@ def tile_phydgalerkinconv_k_kernel(tc, x, wbases, bases, weights, D, out):
         def load_x(b, it):
             nc.sync.dma_start(out=x_sb[b][:, it, :], in_=x[b, it * P : (it + 1) * P, :])
 
+        def load_wbases(b):
+            nc.sync.dma_start(out=wb_sb[b][:], in_=wbases[b].rearrange("(c p) k -> p c k", p=P))
+
         def load_weights(h):
             w_tile = w_in.tile([P, W_CH, KM], BF16, name="w_tile")
             nc.sync.dma_start(
@@ -61,31 +68,26 @@ def tile_phydgalerkinconv_k_kernel(tc, x, wbases, bases, weights, D, out):
             )
             w_sb.append(w_tile)
 
+        def load_bases(b):
+            nc.sync.dma_start(out=bases_sb[b][:], in_=bases[b].rearrange("(c p) k -> p c k", p=P))
+
         d_rows = const.tile([P, PACK, M], BF16)
 
-        def load_the_rest():
-            nc.sync.dma_start(out=wb_sb[1][:], in_=wbases[1].rearrange("(c p) k -> p c k", p=P))
-            for it in range(CH_TILES):
-                load_x(1, it)
-            for b in range(B):
-                nc.sync.dma_start(
-                    out=bases_sb[b][:], in_=bases[b].rearrange("(c p) k -> p c k", p=P)
-                )
-
         load_x(0, 0)
-        nc.sync.dma_start(out=wb_sb[0][:], in_=wbases[0].rearrange("(c p) k -> p c k", p=P))
+        load_wbases(0)
         for q in range(CH_PASS):
             nc.sync.dma_start(
                 out=d_rows[q * REP : (q + 1) * REP, :, :],
                 in_=D.rearrange("(h t) k -> h t k", t=PACK),
             )
-        load_weights(0)
-        load_weights(1)
-        load_x(0, 1)
-        load_weights(2)
-        load_weights(3)
-        load_x(0, 2)
-        load_x(0, 3)
+        load_x(1, 0)
+        load_wbases(1)
+        for it in range(1, CH_TILES):
+            if 2 * it <= W_BUFS:
+                load_weights(2 * it - 2)
+                load_weights(2 * it - 1)
+            load_x(0, it)
+            load_x(1, it)
 
         ident_bf = const.tile([P, P], BF16)
         make_identity(nc, ident_bf[:])
@@ -100,53 +102,23 @@ def tile_phydgalerkinconv_k_kernel(tc, x, wbases, bases, weights, D, out):
         b_codes = [keep.tile([P, N], U32, align_bytes=64, name="b_codes%d" % b) for b in range(B)]
         b_scales = [keep.tile([P, N], U8, align_bytes=64, name="b_scales%d" % b) for b in range(B)]
 
-        def quantise_weights(h):
-            words = (
-                w_sb[h][:]
-                .rearrange("o i j -> o (i j)")
-                .bitcast(F32)
-                .rearrange("o (g p u) -> o g p u", g=W_PASSES, p=P, u=2)
-            )
-            w_grouped = work.tile([P, W_PASSES, CO, PACK], BF16, align_bytes=64)
-            for half in range(W_PASSES // 2):
-                wT_ps = tr_psum.tile([P, 2, 2, CO], F32, tag="tr")
-                for gg in range(2):
-                    for u in range(2):
-                        nc.tensor.transpose(
-                            wT_ps[:, gg, u, :], words[:, 2 * half + gg, :, u], ident_f32[:]
-                        )
-                nc.scalar.copy(
-                    out=w_grouped[:, 2 * half : 2 * half + 2, :, :].bitcast(F32),
-                    in_=wT_ps[:].rearrange("p g u o -> p g o u"),
-                )
-            passes = slice(h * W_PASSES, (h + 1) * W_PASSES)
-            nc.vector.quantize_mx(
-                out=w_codes[:, passes, :].rearrange("p g o -> p (g o)").bitcast(FP8X4),
-                scales=w_scales[:, passes, :].rearrange("p g o -> p (g o)"),
-                in_=w_grouped[:].rearrange("p g o t -> p (g o t)"),
-            )
+        x_hat_t = {}
+        wide = {}
+        z_bf = {}
+        z_mx = {}
+        w_grouped = {}
+        b_grouped = {}
+        y_grouped = {}
+        y_mx = {}
+        acc = {}
 
-        def quantise_bases(b):
-            words = bases_sb[b][:].bitcast(F32)
-            b_grouped = work.tile([P, N_CHUNKS, P, PACK], BF16, align_bytes=64)
-            for pair in range(N_CHUNKS // 2):
-                bT_ps = tr_psum.tile([P, 2, 2, P], F32, tag="tr")
-                for cc in range(2):
-                    for u in range(2):
-                        nc.tensor.transpose(
-                            bT_ps[:, cc, u, :],
-                            words[:, 2 * pair + cc, u * P : (u + 1) * P],
-                            ident_f32[:],
-                        )
-                nc.scalar.copy(
-                    out=b_grouped[:, 2 * pair : 2 * pair + 2, :, :].bitcast(F32),
-                    in_=bT_ps[:].rearrange("p c u n -> p c n u"),
-                )
-            nc.vector.quantize_mx(
-                out=b_codes[b][:].bitcast(FP8X4),
-                scales=b_scales[b][:],
-                in_=b_grouped[:].rearrange("p c n t -> p (c n t)"),
-            )
+        def on_gpsimd(s):
+            return s % ROUND == ROUND - 1
+
+        def where(s):
+            tile_no, gl = divmod(s, TILE_PASSES)
+            it, b = divmod(tile_no, B)
+            return b, it, gl
 
         def project_channels(b, it):
             xT_ps = tr_psum.tile([P, N_CHUNKS, P], BF16, tag="tr")
@@ -164,41 +136,66 @@ def tile_phydgalerkinconv_k_kernel(tc, x, wbases, bases, weights, D, out):
                         start=(c == 0),
                         stop=(c == N_CHUNKS - 1),
                     )
-            x_rep = work.tile([P, TILE_PASSES, M_CHUNKS, CH_PASS, REP], F32)
-            for gl in range(TILE_PASSES):
-                nc.scalar.copy(
-                    out=x_rep[:, gl, :, :, :],
-                    in_=xh_ps[:, :, gl * CH_PASS : (gl + 1) * CH_PASS]
-                    .unsqueeze(3)
-                    .to_broadcast([P, M_CHUNKS, CH_PASS, REP]),
-                )
-            return x_rep
+            xh_sb = work.tile([P, M_CHUNKS, P], F32)
+            nc.scalar.copy(out=xh_sb[:], in_=xh_ps[:])
+            x_hat_t[(b, it)] = xh_sb
 
-        def contract_pass(b, g, x_rep, acc):
-            gl = g % TILE_PASSES
-            x_wide = rep_psum.tile([P, M], F32)
+        def widen(s):
+            b, it, gl = where(s)
+            x_rep = wide_pool.tile([P, M_CHUNKS, CH_PASS, REP], F32)
+            nc.scalar.copy(
+                out=x_rep[:],
+                in_=x_hat_t[(b, it)][:, :, gl * CH_PASS : (gl + 1) * CH_PASS]
+                .unsqueeze(3)
+                .to_broadcast([P, M_CHUNKS, CH_PASS, REP]),
+            )
+            x_wide = wide_psum.tile([P, M], F32)
             for kc in range(M_CHUNKS):
                 nc.tensor.transpose(
                     x_wide[:, kc * P : (kc + 1) * P],
-                    x_rep[:, gl, kc, :, :].rearrange("p i r -> p (i r)"),
+                    x_rep[:, kc, :, :].rearrange("p i r -> p (i r)"),
                     ident_f32[:],
                 )
-            z_bf = z_pool.tile([P, M, PACK], BF16, align_bytes=64)
-            nc.vector.tensor_tensor(
-                out=z_bf[:],
-                in0=x_wide[:].unsqueeze(2).to_broadcast([P, M, PACK]),
+            wide[s] = x_wide
+            if on_gpsimd(s):
+                x_wide_sb = wide_pool.tile([P, M], F32, bufs=2)
+                nc.scalar.copy(out=x_wide_sb[:], in_=x_wide[:])
+                wide[s] = x_wide_sb
+
+        def multiply(s):
+            if on_gpsimd(s):
+                z_tile = z_pool.tile([P, M, PACK], BF16, align_bytes=64, name="z_gpsimd", bufs=1)
+                engine = nc.gpsimd
+            else:
+                z_tile = z_pool.tile([P, M, PACK], BF16, align_bytes=64, name="z_vector", bufs=ROUND)
+                engine = nc.vector
+            engine.tensor_tensor(
+                out=z_tile[:],
+                in0=wide[s][:].unsqueeze(2).to_broadcast([P, M, PACK]),
                 in1=d_grouped[:],
                 op=MULT,
             )
+            z_bf[s] = z_tile
+
+        def quantise(s):
             z_codes = z_pool.tile([P, M], U32, align_bytes=64)
             z_scales = z_pool.tile([P, M], U8, align_bytes=64)
             nc.vector.quantize_mx(
                 out=z_codes[:].bitcast(FP8X4),
                 scales=z_scales[:],
-                in_=z_bf[:].rearrange("p k t -> p (k t)"),
+                in_=z_bf[s][:].rearrange("p k t -> p (k t)"),
             )
+            z_mx[s] = (z_codes, z_scales)
+
+        def contract(s):
+            b, it, gl = where(s)
+            g = it * TILE_PASSES + gl
+            if g == 0:
+                acc_tile = acc_psum.tile([P, M], F32, name="acc%d" % b)
+                acc[b] = acc_tile
+            z_codes, z_scales = z_mx[s]
             nc.tensor.matmul_mx(
-                out=acc[:],
+                out=acc[b][:],
                 lhsT=w_codes[:, g, :].bitcast(FP8X4),
                 lhsT_scale=w_scales[:, g, :],
                 rhs=z_codes[:].bitcast(FP8X4),
@@ -207,23 +204,84 @@ def tile_phydgalerkinconv_k_kernel(tc, x, wbases, bases, weights, D, out):
                 stop=(g == PASSES - 1),
             )
 
-        def reconstruct(b, acc):
+        def regroup_weights(h):
+            words = (
+                w_sb[h][:]
+                .rearrange("o i j -> o (i j)")
+                .bitcast(F32)
+                .rearrange("o (g p u) -> o g p u", g=W_PASSES, p=P, u=2)
+            )
+            grouped = work.tile([P, W_PASSES, CO, PACK], BF16, align_bytes=64, name="w_grouped")
+            for half in range(W_PASSES // 2):
+                wT_ps = tr_psum.tile([P, 2, 2, CO], F32, tag="tr")
+                for gg in range(2):
+                    for u in range(2):
+                        nc.tensor.transpose(
+                            wT_ps[:, gg, u, :], words[:, 2 * half + gg, :, u], ident_f32[:]
+                        )
+                nc.scalar.copy(
+                    out=grouped[:, 2 * half : 2 * half + 2, :, :].bitcast(F32),
+                    in_=wT_ps[:].rearrange("p g u o -> p g o u"),
+                )
+            w_grouped[h] = grouped
+
+        def quantise_weights(h):
+            passes = slice(h * W_PASSES, (h + 1) * W_PASSES)
+            nc.vector.quantize_mx(
+                out=w_codes[:, passes, :].rearrange("p g o -> p (g o)").bitcast(FP8X4),
+                scales=w_scales[:, passes, :].rearrange("p g o -> p (g o)"),
+                in_=w_grouped[h][:].rearrange("p g o t -> p (g o t)"),
+            )
+
+        def regroup_bases(b):
+            words = bases_sb[b][:].bitcast(F32)
+            grouped = work.tile([P, N_CHUNKS, P, PACK], BF16, align_bytes=64, name="b_grouped")
+            for pair in range(N_CHUNKS // 2):
+                bT_ps = tr_psum.tile([P, 2, 2, P], F32, tag="tr")
+                for cc in range(2):
+                    for u in range(2):
+                        nc.tensor.transpose(
+                            bT_ps[:, cc, u, :],
+                            words[:, 2 * pair + cc, u * P : (u + 1) * P],
+                            ident_f32[:],
+                        )
+                nc.scalar.copy(
+                    out=grouped[:, 2 * pair : 2 * pair + 2, :, :].bitcast(F32),
+                    in_=bT_ps[:].rearrange("p c u n -> p c n u"),
+                )
+            b_grouped[b] = grouped
+
+        def quantise_bases(b):
+            nc.vector.quantize_mx(
+                out=b_codes[b][:].bitcast(FP8X4),
+                scales=b_scales[b][:],
+                in_=b_grouped[b][:].rearrange("p c n t -> p (c n t)"),
+            )
+
+        def regroup_y_hat(b):
             y_sb = work.tile([P, M], F32)
-            nc.scalar.copy(out=y_sb[:], in_=acc[:])
+            nc.scalar.copy(out=y_sb[:], in_=acc[b][:])
             y_cols = y_sb[:].rearrange("o (u p e) -> o u e p", u=2, p=P, e=2)
             yT_ps = tr_psum.tile([P, PACK, CO], F32, tag="tr")
             for u in range(2):
                 for e in range(2):
                     nc.tensor.transpose(yT_ps[:, 2 * u + e, :], y_cols[:, u, e, :], ident_f32[:])
-            y_grouped = work.tile([P, CO, PACK], BF16, align_bytes=64)
-            nc.scalar.copy(out=y_grouped[:], in_=yT_ps[:].rearrange("p t o -> p o t"))
+            grouped = work.tile([P, CO, PACK], BF16, align_bytes=64, name="y_grouped")
+            nc.scalar.copy(out=grouped[:], in_=yT_ps[:].rearrange("p t o -> p o t"))
+            y_grouped[b] = grouped
+
+        def quantise_y_hat(b):
             y_codes = work.tile([P, CO], U32, align_bytes=64)
             y_scales = work.tile([P, CO], U8, align_bytes=64)
             nc.vector.quantize_mx(
                 out=y_codes[:].bitcast(FP8X4),
                 scales=y_scales[:],
-                in_=y_grouped[:].rearrange("p o t -> p (o t)"),
+                in_=y_grouped[b][:].rearrange("p o t -> p (o t)"),
             )
+            y_mx[b] = (y_codes, y_scales)
+
+        def reconstruct(b):
+            y_codes, y_scales = y_mx[b]
             for half in range(N // N_HALF):
                 cols = slice(half * N_HALF, (half + 1) * N_HALF)
                 o_ps = tr_psum.tile([P, N_HALF], F32, tag="tr")
@@ -240,20 +298,66 @@ def tile_phydgalerkinconv_k_kernel(tc, x, wbases, bases, weights, D, out):
                 nc.scalar.copy(out=o_sb[:], in_=o_ps[:])
                 nc.sync.dma_start(out=out[b, :, cols], in_=o_sb[:])
 
-        for b in range(B):
-            acc = acc_psum.tile([P, M], F32)
-            for it in range(CH_TILES):
-                x_rep = project_channels(b, it)
-                for gl in range(TILE_PASSES):
-                    g = it * TILE_PASSES + gl
-                    if b == 0 and g % W_PASSES == 0:
-                        h = g // W_PASSES
-                        quantise_weights(h)
-                        if h + W_BUFS < W_LOADS:
-                            load_weights(h + W_BUFS)
-                        if h + W_BUFS == W_LOADS - 1:
-                            load_the_rest()
-                    contract_pass(b, g, x_rep, acc)
-                if it == CH_TILES - 2:
+        def passes_of(r):
+            return [s for s in range(r * ROUND, (r + 1) * ROUND) if 0 <= s < ALL_PASSES]
+
+        def gpsimd_first(passes):
+            return [s for s in passes if on_gpsimd(s)] + [s for s in passes if not on_gpsimd(s)]
+
+        def project_for(passes):
+            for s in passes:
+                b, it, gl = where(s)
+                if gl == 0:
+                    project_channels(b, it)
+
+        def regroup_for(passes):
+            for s in passes:
+                b, it, gl = where(s)
+                if b == 0 and gl % W_PASSES == 0:
+                    h = (it * TILE_PASSES + gl) // W_PASSES
+                    regroup_weights(h)
+                    if h + W_BUFS < W_LOADS:
+                        load_weights(h + W_BUFS)
+                    if h + W_BUFS == W_LOADS - 1:
+                        load_bases(0)
+                        load_bases(1)
+                if it == CH_TILES - 2 and gl == 0:
+                    regroup_bases(b)
+
+        def is_last(s):
+            b, it, gl = where(s)
+            return it == CH_TILES - 1 and gl == TILE_PASSES - 1
+
+        def quantise_for(passes):
+            for s in passes:
+                b, it, gl = where(s)
+                if b == 0 and gl % W_PASSES == 0:
+                    quantise_weights((it * TILE_PASSES + gl) // W_PASSES)
+                if it == CH_TILES - 2 and gl == 0:
                     quantise_bases(b)
-            reconstruct(b, acc)
+
+        project_for(passes_of(0) + passes_of(1))
+        for s in gpsimd_first(passes_of(0)):
+            widen(s)
+
+        rounds = (ALL_PASSES + ROUND - 1) // ROUND
+        for r in range(rounds + 2):
+            for s in gpsimd_first(passes_of(r + 1)):
+                widen(s)
+            project_for(passes_of(r + 2))
+            regroup_for(passes_of(r))
+            for s in gpsimd_first(passes_of(r)):
+                multiply(s)
+            quantise_for(passes_of(r - 1))
+            for s in passes_of(r - 2):
+                if is_last(s):
+                    quantise_y_hat(where(s)[0])
+            for s in passes_of(r):
+                quantise(s)
+            for s in passes_of(r - 1):
+                contract(s)
+                if is_last(s):
+                    regroup_y_hat(where(s)[0])
+            for s in passes_of(r - 2):
+                if is_last(s):
+                    reconstruct(where(s)[0])

@@ -28,7 +28,8 @@ W_CH = W_PASSES * CH_PASS
 W_LOADS = PASSES // W_PASSES
 W_BUFS = 4
 N_HALF = 512
-ROUND = 3
+ROUND = 4
+WIDE_BANKS = 3
 
 FLOPS = 2 * B * (CI * N * M + CI * KM * CO * M + CO * M * N)
 
@@ -45,7 +46,7 @@ def tile_phydgalerkinconv_k_kernel(tc, x, wbases, bases, weights, D, out):
         wide_pool = ctx.enter_context(tc.tile_pool(name="wide_pool", bufs=ROUND))
         z_pool = ctx.enter_context(tc.tile_pool(name="z_pool", bufs=2 * ROUND))
         acc_psum = ctx.enter_context(tc.psum_pool(name="acc_psum", bufs=1))
-        wide_psum = ctx.enter_context(tc.psum_pool(name="wide_psum", bufs=ROUND))
+        wide_psum = ctx.enter_context(tc.psum_pool(name="wide_psum", bufs=WIDE_BANKS))
         xh_psum = ctx.enter_context(tc.psum_pool(name="xh_psum", bufs=1))
         tr_psum = ctx.enter_context(tc.psum_pool(name="tr_psum", bufs=2))
 

@@ -76,10 +76,10 @@ def tile_phydgalerkinconv_k_kernel(tc, x, wbases, bases, weights, D, out):
 
         load_x(0, 0)
         load_wbases(0)
-        for q in range(CH_PASS):
+        for h in range(REP):
             nc.sync.dma_start(
-                out=d_rows[q * REP : (q + 1) * REP, :, :],
-                in_=D.rearrange("(h t) k -> h t k", t=PACK),
+                out=d_rows[h:P:REP, :, :],
+                in_=D[h * PACK : (h + 1) * PACK, :].unsqueeze(0).to_broadcast([CH_PASS, PACK, M]),
             )
         load_x(1, 0)
         load_wbases(1)
@@ -235,7 +235,7 @@ def tile_phydgalerkinconv_k_kernel(tc, x, wbases, bases, weights, D, out):
             )
 
         def regroup_bases(b):
-            words = bases_sb[b][:].bitcast(F32)
+            words = bases_sb[b][:].bitcast(F32).rearrange("n c (p u) -> n c p u", u=2)
             grouped = work.tile([P, N_CHUNKS, P, PACK], BF16, align_bytes=64, name="b_grouped")
             for pair in range(N_CHUNKS // 2):
                 bT_ps = tr_psum.tile([P, 2, 2, P], F32, tag="tr")
@@ -243,7 +243,7 @@ def tile_phydgalerkinconv_k_kernel(tc, x, wbases, bases, weights, D, out):
                     for u in range(2):
                         nc.tensor.transpose(
                             bT_ps[:, cc, u, :],
-                            words[:, 2 * pair + cc, u * P : (u + 1) * P],
+                            words[:, 2 * pair + cc, :, u],
                             ident_f32[:],
                         )
                 nc.scalar.copy(
@@ -262,11 +262,10 @@ def tile_phydgalerkinconv_k_kernel(tc, x, wbases, bases, weights, D, out):
         def regroup_y_hat(b):
             y_sb = work.tile([P, M], F32)
             nc.scalar.copy(out=y_sb[:], in_=acc[b][:])
-            y_cols = y_sb[:].rearrange("o (u p e) -> o u e p", u=2, p=P, e=2)
+            y_cols = y_sb[:].rearrange("o (p t) -> o t p", t=PACK)
             yT_ps = tr_psum.tile([P, PACK, CO], F32, tag="tr")
-            for u in range(2):
-                for e in range(2):
-                    nc.tensor.transpose(yT_ps[:, 2 * u + e, :], y_cols[:, u, e, :], ident_f32[:])
+            for t in range(PACK):
+                nc.tensor.transpose(yT_ps[:, t, :], y_cols[:, t, :], ident_f32[:])
             grouped = work.tile([P, CO, PACK], BF16, align_bytes=64, name="y_grouped")
             nc.scalar.copy(out=grouped[:], in_=yT_ps[:].rearrange("p t o -> p o t"))
             y_grouped[b] = grouped

@@ -31,6 +31,8 @@ N_HALF = 512
 ROUND = 4
 WIDE_BANKS = 3
 
+assert TILE_PASSES % ROUND == 0
+
 FLOPS = 2 * B * (CI * N * M + CI * KM * CO * M + CO * M * N)
 
 
@@ -43,7 +45,7 @@ def tile_phydgalerkinconv_k_kernel(tc, x, wbases, bases, weights, D, out):
         w_in = ctx.enter_context(tc.tile_pool(name="w_in", bufs=W_BUFS))
         keep = ctx.enter_context(tc.tile_pool(name="keep", bufs=1))
         work = ctx.enter_context(tc.tile_pool(name="work", bufs=2))
-        wide_pool = ctx.enter_context(tc.tile_pool(name="wide_pool", bufs=ROUND))
+        wide_pool = ctx.enter_context(tc.tile_pool(name="wide_pool", bufs=2 * ROUND))
         z_pool = ctx.enter_context(tc.tile_pool(name="z_pool", bufs=2 * ROUND))
         acc_psum = ctx.enter_context(tc.psum_pool(name="acc_psum", bufs=1))
         wide_psum = ctx.enter_context(tc.psum_pool(name="wide_psum", bufs=WIDE_BANKS))
@@ -103,7 +105,8 @@ def tile_phydgalerkinconv_k_kernel(tc, x, wbases, bases, weights, D, out):
         b_codes = [keep.tile([P, N], U32, align_bytes=64, name="b_codes%d" % b) for b in range(B)]
         b_scales = [keep.tile([P, N], U8, align_bytes=64, name="b_scales%d" % b) for b in range(B)]
 
-        x_hat_t = {}
+        x_t = {}
+        x_rep = {}
         wide = {}
         z_bf = {}
         z_mx = {}
@@ -116,45 +119,58 @@ def tile_phydgalerkinconv_k_kernel(tc, x, wbases, bases, weights, D, out):
         def on_gpsimd(s):
             return s % ROUND == ROUND - 1
 
+        def passes_of(r):
+            return [s for s in range(r * ROUND, (r + 1) * ROUND) if 0 <= s < ALL_PASSES]
+
+        def gpsimd_first(passes):
+            return [s for s in passes if on_gpsimd(s)] + [s for s in passes if not on_gpsimd(s)]
+
         def where(s):
             tile_no, gl = divmod(s, TILE_PASSES)
             it, b = divmod(tile_no, B)
             return b, it, gl
 
-        def project_channels(b, it):
+        def transpose_x(b, it):
             xT_ps = tr_psum.tile([P, N_CHUNKS, P], BF16, tag="tr")
             for c in range(N_CHUNKS):
                 nc.tensor.transpose(xT_ps[:, c, :], x_sb[b][:, it, c * P : (c + 1) * P], ident_bf[:])
             xT_sb = work.tile([P, N_CHUNKS, P], BF16)
             nc.scalar.copy(out=xT_sb[:], in_=xT_ps[:])
-            xh_ps = xh_psum.tile([P, M_CHUNKS, P], F32)
+            x_t[(b, it)] = xT_sb
+
+        def project(r):
+            if not passes_of(r):
+                return
+            b, it, gl = where(r * ROUND)
+            if gl == 0:
+                transpose_x(b, it)
+            channels = slice(gl * CH_PASS, (gl + ROUND) * CH_PASS)
+            xh_ps = xh_psum.tile([P, M_CHUNKS, ROUND, CH_PASS], F32)
             for kc in range(M_CHUNKS):
                 for c in range(N_CHUNKS):
                     nc.tensor.matmul(
-                        xh_ps[:, kc, :],
+                        xh_ps[:, kc, :, :].rearrange("p g i -> p (g i)"),
                         lhsT=wb_sb[b][:, c, kc * P : (kc + 1) * P],
-                        rhs=xT_sb[:, c, :],
+                        rhs=x_t[(b, it)][:, c, channels],
                         start=(c == 0),
                         stop=(c == N_CHUNKS - 1),
                     )
-            xh_sb = work.tile([P, M_CHUNKS, P], F32)
-            nc.scalar.copy(out=xh_sb[:], in_=xh_ps[:])
-            x_hat_t[(b, it)] = xh_sb
+            for s in gpsimd_first(passes_of(r)):
+                rep_tile = wide_pool.tile([P, M_CHUNKS, CH_PASS, REP], F32, name="x_rep")
+                nc.scalar.copy(
+                    out=rep_tile[:],
+                    in_=xh_ps[:, :, s % ROUND, :]
+                    .unsqueeze(3)
+                    .to_broadcast([P, M_CHUNKS, CH_PASS, REP]),
+                )
+                x_rep[s] = rep_tile
 
         def widen(s):
-            b, it, gl = where(s)
-            x_rep = wide_pool.tile([P, M_CHUNKS, CH_PASS, REP], F32)
-            nc.scalar.copy(
-                out=x_rep[:],
-                in_=x_hat_t[(b, it)][:, :, gl * CH_PASS : (gl + 1) * CH_PASS]
-                .unsqueeze(3)
-                .to_broadcast([P, M_CHUNKS, CH_PASS, REP]),
-            )
             x_wide = wide_psum.tile([P, M], F32)
             for kc in range(M_CHUNKS):
                 nc.tensor.transpose(
                     x_wide[:, kc * P : (kc + 1) * P],
-                    x_rep[:, kc, :, :].rearrange("p i r -> p (i r)"),
+                    x_rep[s][:, kc, :, :].rearrange("p i r -> p (i r)"),
                     ident_f32[:],
                 )
             wide[s] = x_wide
@@ -298,18 +314,6 @@ def tile_phydgalerkinconv_k_kernel(tc, x, wbases, bases, weights, D, out):
                 nc.scalar.copy(out=o_sb[:], in_=o_ps[:])
                 nc.sync.dma_start(out=out[b, :, cols], in_=o_sb[:])
 
-        def passes_of(r):
-            return [s for s in range(r * ROUND, (r + 1) * ROUND) if 0 <= s < ALL_PASSES]
-
-        def gpsimd_first(passes):
-            return [s for s in passes if on_gpsimd(s)] + [s for s in passes if not on_gpsimd(s)]
-
-        def project_for(passes):
-            for s in passes:
-                b, it, gl = where(s)
-                if gl == 0:
-                    project_channels(b, it)
-
         def regroup_for(passes):
             for s in passes:
                 b, it, gl = where(s)
@@ -333,19 +337,19 @@ def tile_phydgalerkinconv_k_kernel(tc, x, wbases, bases, weights, D, out):
                 b, it, gl = where(s)
                 if b == 0 and gl % W_PASSES == 0:
                     quantise_weights((it * TILE_PASSES + gl) // W_PASSES)
-                if it == CH_TILES - 2 and gl == 0:
+                if it == CH_TILES - 2 and gl == ROUND:
                     quantise_bases(b)
 
-        project_for(passes_of(0) + passes_of(1))
+        project(0)
         for s in gpsimd_first(passes_of(0)):
             widen(s)
+        project(1)
 
         rounds = (ALL_PASSES + ROUND - 1) // ROUND
         for r in range(rounds + 2):
             for s in gpsimd_first(passes_of(r + 1)):
                 widen(s)
-            project_for(passes_of(r + 2))
-            regroup_for(passes_of(r))
+            project(r + 2)
             for s in gpsimd_first(passes_of(r)):
                 multiply(s)
             quantise_for(passes_of(r - 1))
@@ -361,3 +365,4 @@ def tile_phydgalerkinconv_k_kernel(tc, x, wbases, bases, weights, D, out):
             for s in passes_of(r - 2):
                 if is_last(s):
                     reconstruct(where(s)[0])
+            regroup_for(passes_of(r))

@@ -9,6 +9,8 @@ U32 = mybir.dt.uint32
 U8 = mybir.dt.uint8
 FP8X4 = mybir.dt.float8_e4m3fn_x4
 MULT = mybir.AluOpType.mult
+ADD = mybir.AluOpType.add
+COPY = mybir.ActivationFunctionType.Copy
 
 B, CI, CO, N, KM, M = 2, 512, 128, 1024, 32, 512
 
@@ -18,20 +20,24 @@ K_PASS = P * PACK
 CH_PASS = K_PASS // KM
 REP = P // CH_PASS
 PASSES = CI // CH_PASS
-ALL_PASSES = B * PASSES
-CH_TILES = CI // P
 TILE_PASSES = P // CH_PASS
 N_CHUNKS = N // P
 M_CHUNKS = M // P
 W_PASSES = 4
 W_CH = W_PASSES * CH_PASS
-W_LOADS = PASSES // W_PASSES
 W_BUFS = 4
 N_HALF = 512
 ROUND = 4
 WIDE_BANKS = 3
 
-assert TILE_PASSES % ROUND == 0
+WIDE_TILES = 3
+TURNED_TILE = WIDE_TILES
+WIDE_PASSES = B * WIDE_TILES * TILE_PASSES
+CLASSES = 4
+QUADS = P // CLASSES
+TURN_ROUNDS = TILE_PASSES // ROUND
+SLOT_COLUMNS = 1024
+ON_GPSIMD = 6
 
 FLOPS = 2 * B * (CI * N * M + CI * KM * CO * M + CO * M * N)
 
@@ -42,6 +48,7 @@ def tile_phydgalerkinconv_k_kernel(tc, x, wbases, bases, weights, D, out):
         ctx.enter_context(tc.manual_schedule())
         const = ctx.enter_context(tc.tile_pool(name="const", bufs=1))
         inputs = ctx.enter_context(tc.tile_pool(name="inputs", bufs=1))
+        inbox = ctx.enter_context(tc.tile_pool(name="inbox", bufs=10))
         w_in = ctx.enter_context(tc.tile_pool(name="w_in", bufs=W_BUFS))
         keep = ctx.enter_context(tc.tile_pool(name="keep", bufs=1))
         work = ctx.enter_context(tc.tile_pool(name="work", bufs=2))
@@ -52,13 +59,15 @@ def tile_phydgalerkinconv_k_kernel(tc, x, wbases, bases, weights, D, out):
         xh_psum = ctx.enter_context(tc.psum_pool(name="xh_psum", bufs=1))
         tr_psum = ctx.enter_context(tc.psum_pool(name="tr_psum", bufs=2))
 
-        x_sb = [inputs.tile([P, CH_TILES, N], BF16, name="x_sb%d" % b) for b in range(B)]
+        x_sb = {}
+        bases_sb = {}
+        w_sb = {}
         wb_sb = [inputs.tile([P, N_CHUNKS, M], BF16, name="wb_sb%d" % b) for b in range(B)]
-        bases_sb = [inputs.tile([P, N_CHUNKS, M], BF16, name="bases_sb%d" % b) for b in range(B)]
-        w_sb = []
 
         def load_x(b, it):
-            nc.sync.dma_start(out=x_sb[b][:, it, :], in_=x[b, it * P : (it + 1) * P, :])
+            in_tile = inbox.tile([P, N], BF16)
+            nc.sync.dma_start(out=in_tile[:], in_=x[b, it * P : (it + 1) * P, :])
+            x_sb[(b, it)] = in_tile
 
         def load_wbases(b):
             nc.sync.dma_start(out=wb_sb[b][:], in_=wbases[b].rearrange("(c p) k -> p c k", p=P))
@@ -69,12 +78,19 @@ def tile_phydgalerkinconv_k_kernel(tc, x, wbases, bases, weights, D, out):
                 out=w_tile[:],
                 in_=weights[h * W_CH : (h + 1) * W_CH, :, :].rearrange("i o j -> o i j"),
             )
-            w_sb.append(w_tile)
+            w_sb[h] = w_tile
 
-        def load_bases(b):
-            nc.sync.dma_start(out=bases_sb[b][:], in_=bases[b].rearrange("(c p) k -> p c k", p=P))
+        def load_bases(b, pair):
+            in_tile = inbox.tile([P, 2, M], BF16)
+            nc.sync.dma_start(
+                out=in_tile[:],
+                in_=bases[b, 2 * pair * P : 2 * (pair + 1) * P, :].rearrange("(c p) k -> p c k", p=P),
+            )
+            bases_sb[(b, pair)] = in_tile
 
-        d_rows = const.tile([P, PACK, M], BF16)
+        d_rows = work.tile([P, PACK, M], BF16, align_bytes=64, name="b_grouped")
+
+        w_order = [0, 1, 6, 7, 2, 3, 4, 5]
 
         load_x(0, 0)
         load_wbases(0)
@@ -83,14 +99,26 @@ def tile_phydgalerkinconv_k_kernel(tc, x, wbases, bases, weights, D, out):
                 out=d_rows[h:P:REP, :, :],
                 in_=D[h * PACK : (h + 1) * PACK, :].unsqueeze(0).to_broadcast([CH_PASS, PACK, M]),
             )
+        load_x(0, TURNED_TILE)
         load_x(1, 0)
         load_wbases(1)
-        for it in range(1, CH_TILES):
-            if 2 * it <= W_BUFS:
-                load_weights(2 * it - 2)
-                load_weights(2 * it - 1)
-            load_x(0, it)
-            load_x(1, it)
+        load_weights(w_order[0])
+        load_weights(w_order[1])
+        load_x(1, TURNED_TILE)
+        load_x(0, 1)
+        load_weights(w_order[2])
+        load_weights(w_order[3])
+        load_x(1, 1)
+        load_x(0, 2)
+        load_x(1, 2)
+        load_bases(0, 0)
+        load_bases(0, 1)
+        w_loaded = [W_BUFS]
+
+        def load_next_weights():
+            if w_loaded[0] < len(w_order):
+                load_weights(w_order[w_loaded[0]])
+                w_loaded[0] = w_loaded[0] + 1
 
         ident_bf = const.tile([P, P], BF16)
         make_identity(nc, ident_bf[:])
@@ -105,7 +133,12 @@ def tile_phydgalerkinconv_k_kernel(tc, x, wbases, bases, weights, D, out):
         b_codes = [keep.tile([P, N], U32, align_bytes=64, name="b_codes%d" % b) for b in range(B)]
         b_scales = [keep.tile([P, N], U8, align_bytes=64, name="b_scales%d" % b) for b in range(B)]
 
+        d_t = const.tile([P, M_CHUNKS, KM], F32)
+        xh_t = {}
+        z_t = {}
+
         x_t = {}
+        xh = {}
         x_rep = {}
         wide = {}
         z_bf = {}
@@ -115,12 +148,14 @@ def tile_phydgalerkinconv_k_kernel(tc, x, wbases, bases, weights, D, out):
         y_grouped = {}
         y_mx = {}
         acc = {}
+        done = {0: 0, 1: 0}
+        finished = {}
 
         def on_gpsimd(s):
             return s % ROUND == ROUND - 1
 
         def passes_of(r):
-            return [s for s in range(r * ROUND, (r + 1) * ROUND) if 0 <= s < ALL_PASSES]
+            return [s for s in range(r * ROUND, (r + 1) * ROUND) if 0 <= s < WIDE_PASSES]
 
         def gpsimd_first(passes):
             return [s for s in passes if on_gpsimd(s)] + [s for s in passes if not on_gpsimd(s)]
@@ -130,36 +165,46 @@ def tile_phydgalerkinconv_k_kernel(tc, x, wbases, bases, weights, D, out):
             it, b = divmod(tile_no, B)
             return b, it, gl
 
-        def transpose_x(b, it):
+        def transpose_x(b, it, pool_name):
             xT_ps = tr_psum.tile([P, N_CHUNKS, P], BF16, tag="tr")
             for c in range(N_CHUNKS):
-                nc.tensor.transpose(xT_ps[:, c, :], x_sb[b][:, it, c * P : (c + 1) * P], ident_bf[:])
-            xT_sb = work.tile([P, N_CHUNKS, P], BF16)
+                nc.tensor.transpose(xT_ps[:, c, :], x_sb[(b, it)][:, c * P : (c + 1) * P], ident_bf[:])
+            xT_sb = work.tile([P, N_CHUNKS, P], BF16, name=pool_name, bufs=1 if pool_name == "xT_turned" else 2)
             nc.scalar.copy(out=xT_sb[:], in_=xT_ps[:])
             x_t[(b, it)] = xT_sb
 
-        def project(r):
-            if not passes_of(r):
+        def starts_tile(r):
+            return len(passes_of(r)) > 0 and where(r * ROUND)[2] == 0
+
+        def prepare(r):
+            if starts_tile(r):
+                b, it, gl = where(r * ROUND)
+                transpose_x(b, it, "xT_sb")
+
+        def project(r, chunks):
+            if not starts_tile(r):
                 return
             b, it, gl = where(r * ROUND)
-            if gl == 0:
-                transpose_x(b, it)
-            channels = slice(gl * CH_PASS, (gl + ROUND) * CH_PASS)
-            xh_ps = xh_psum.tile([P, M_CHUNKS, ROUND, CH_PASS], F32)
-            for kc in range(M_CHUNKS):
+            if chunks[0] == 0:
+                xh_ps = xh_psum.tile([P, M_CHUNKS, TILE_PASSES, CH_PASS], F32)
+                xh[(b, it)] = xh_ps
+            for kc in chunks:
                 for c in range(N_CHUNKS):
                     nc.tensor.matmul(
-                        xh_ps[:, kc, :, :].rearrange("p g i -> p (g i)"),
+                        xh[(b, it)][:, kc, :, :].rearrange("p g i -> p (g i)"),
                         lhsT=wb_sb[b][:, c, kc * P : (kc + 1) * P],
-                        rhs=x_t[(b, it)][:, c, channels],
+                        rhs=x_t[(b, it)][:, c, :],
                         start=(c == 0),
                         stop=(c == N_CHUNKS - 1),
                     )
+
+        def replicate(r):
             for s in gpsimd_first(passes_of(r)):
+                b, it, gl = where(s)
                 rep_tile = wide_pool.tile([P, M_CHUNKS, CH_PASS, REP], F32, name="x_rep")
                 nc.scalar.copy(
                     out=rep_tile[:],
-                    in_=xh_ps[:, :, s % ROUND, :]
+                    in_=xh[(b, it)][:, :, gl, :]
                     .unsqueeze(3)
                     .to_broadcast([P, M_CHUNKS, CH_PASS, REP]),
                 )
@@ -184,7 +229,7 @@ def tile_phydgalerkinconv_k_kernel(tc, x, wbases, bases, weights, D, out):
                 z_tile = z_pool.tile([P, M, PACK], BF16, align_bytes=64, name="z_gpsimd", bufs=1)
                 engine = nc.gpsimd
             else:
-                z_tile = z_pool.tile([P, M, PACK], BF16, align_bytes=64, name="z_vector", bufs=ROUND)
+                z_tile = z_pool.tile([P, M, PACK], BF16, align_bytes=64, name="z_vector", bufs=ROUND - 1)
                 engine = nc.vector
             engine.tensor_tensor(
                 out=z_tile[:],
@@ -195,8 +240,9 @@ def tile_phydgalerkinconv_k_kernel(tc, x, wbases, bases, weights, D, out):
             z_bf[s] = z_tile
 
         def quantise(s):
-            z_codes = z_pool.tile([P, M], U32, align_bytes=64)
-            z_scales = z_pool.tile([P, M], U8, align_bytes=64)
+            turned = s not in wide
+            z_codes = z_pool.tile([P, M], U32, align_bytes=64, name="zt_codes" if turned else "z_codes", bufs=ROUND if turned else 2 * ROUND)
+            z_scales = z_pool.tile([P, M], U8, align_bytes=64, name="zt_scales" if turned else "z_scales", bufs=ROUND if turned else 2 * ROUND)
             nc.vector.quantize_mx(
                 out=z_codes[:].bitcast(FP8X4),
                 scales=z_scales[:],
@@ -204,10 +250,8 @@ def tile_phydgalerkinconv_k_kernel(tc, x, wbases, bases, weights, D, out):
             )
             z_mx[s] = (z_codes, z_scales)
 
-        def contract(s):
-            b, it, gl = where(s)
-            g = it * TILE_PASSES + gl
-            if g == 0:
+        def contract(s, b, g, r):
+            if done[b] == 0:
                 acc_tile = acc_psum.tile([P, M], F32, name="acc%d" % b)
                 acc[b] = acc_tile
             z_codes, z_scales = z_mx[s]
@@ -217,9 +261,13 @@ def tile_phydgalerkinconv_k_kernel(tc, x, wbases, bases, weights, D, out):
                 lhsT_scale=w_scales[:, g, :],
                 rhs=z_codes[:].bitcast(FP8X4),
                 rhs_scale=z_scales[:],
-                start=(g == 0),
-                stop=(g == PASSES - 1),
+                start=(done[b] == 0),
+                stop=(done[b] == PASSES - 1),
             )
+            done[b] = done[b] + 1
+            if done[b] == PASSES:
+                regroup_y_hat(b)
+                finished[b] = r
 
         def regroup_weights(h):
             words = (
@@ -250,33 +298,30 @@ def tile_phydgalerkinconv_k_kernel(tc, x, wbases, bases, weights, D, out):
                 in_=w_grouped[h][:].rearrange("p g o t -> p (g o t)"),
             )
 
-        def regroup_bases(b):
-            words = bases_sb[b][:].bitcast(F32).rearrange("n c (p u) -> n c p u", u=2)
-            grouped = work.tile([P, N_CHUNKS, P, PACK], BF16, align_bytes=64, name="b_grouped")
-            for pair in range(N_CHUNKS // 2):
+        def regroup_bases(b, half):
+            grouped = work.tile([P, N_CHUNKS // 2, P, PACK], BF16, align_bytes=64, name="b_grouped")
+            for pp in range(2):
+                words = bases_sb[(b, 2 * half + pp)][:].bitcast(F32).rearrange("n c (p u) -> n c p u", u=2)
                 bT_ps = tr_psum.tile([P, 2, 2, P], F32, tag="tr")
                 for cc in range(2):
                     for u in range(2):
-                        nc.tensor.transpose(
-                            bT_ps[:, cc, u, :],
-                            words[:, 2 * pair + cc, :, u],
-                            ident_f32[:],
-                        )
+                        nc.tensor.transpose(bT_ps[:, cc, u, :], words[:, cc, :, u], ident_f32[:])
                 nc.scalar.copy(
-                    out=grouped[:, 2 * pair : 2 * pair + 2, :, :].bitcast(F32),
+                    out=grouped[:, 2 * pp : 2 * pp + 2, :, :].bitcast(F32),
                     in_=bT_ps[:].rearrange("p c u n -> p c n u"),
                 )
-            b_grouped[b] = grouped
+            b_grouped[(b, half)] = grouped
 
-        def quantise_bases(b):
+        def quantise_bases(b, half):
+            cols = slice(half * N_HALF, (half + 1) * N_HALF)
             nc.vector.quantize_mx(
-                out=b_codes[b][:].bitcast(FP8X4),
-                scales=b_scales[b][:],
-                in_=b_grouped[b][:].rearrange("p c n t -> p (c n t)"),
+                out=b_codes[b][:, cols].bitcast(FP8X4),
+                scales=b_scales[b][:, cols],
+                in_=b_grouped[(b, half)][:].rearrange("p c n t -> p (c n t)"),
             )
 
         def regroup_y_hat(b):
-            y_sb = work.tile([P, M], F32)
+            y_sb = work.tile([P, M], F32, name="f32_row")
             nc.scalar.copy(out=y_sb[:], in_=acc[b][:])
             y_cols = y_sb[:].rearrange("o (p t) -> o t p", t=PACK)
             yT_ps = tr_psum.tile([P, PACK, CO], F32, tag="tr")
@@ -310,59 +355,225 @@ def tile_phydgalerkinconv_k_kernel(tc, x, wbases, bases, weights, D, out):
                     start=True,
                     stop=True,
                 )
-                o_sb = work.tile([P, N_HALF], F32)
+                o_sb = work.tile([P, N_HALF], F32, name="f32_row")
                 nc.scalar.copy(out=o_sb[:], in_=o_ps[:])
                 nc.sync.dma_start(out=out[b, :, cols], in_=o_sb[:])
+
+        def transpose_d():
+            for half in range(M_CHUNKS // 2):
+                dT_ps = tr_psum.tile([P, 2, PACK, P], BF16, tag="tr")
+                for cc in range(2):
+                    kc = 2 * half + cc
+                    for t in range(PACK):
+                        nc.tensor.transpose(dT_ps[:, cc, t, :], d_rows[:, t, kc * P : (kc + 1) * P], ident_bf[:])
+                nc.scalar.copy(
+                    out=d_t[:, 2 * half : 2 * half + 2, :].rearrange("k c (p t) -> k c p t", t=PACK),
+                    in_=dT_ps[:, :, :, 0:REP].rearrange("k c t p -> k c p t"),
+                )
+
+        def project_turned(b):
+            xh_ps = xh_psum.tile([P, M_CHUNKS, P], F32)
+            for kc in range(M_CHUNKS):
+                for c in range(N_CHUNKS):
+                    nc.tensor.matmul(
+                        xh_ps[:, kc, :],
+                        lhsT=wb_sb[b][:, c, kc * P : (kc + 1) * P],
+                        rhs=x_t[(b, TURNED_TILE)][:, c, :],
+                        start=(c == 0),
+                        stop=(c == N_CHUNKS - 1),
+                    )
+            xh_tile = work.tile([P, M_CHUNKS, CLASSES, QUADS], F32, name="xh_turned")
+            nc.scalar.copy(out=xh_tile[:], in_=xh_ps[:].rearrange("k c (q r) -> k c r q", r=CLASSES))
+            xh_t[b] = xh_tile
+
+        def multiply_turned(on_scalar, b, kc, j):
+            if j == 0:
+                z_tile = keep.tile([P, CLASSES, KM, QUADS], BF16, name="z_t%d" % kc)
+                z_t[kc] = z_tile
+            if on_scalar:
+                nc.scalar.activation(
+                    out=z_t[kc][:, :, j, :],
+                    in_=xh_t[b][:, kc, :, :],
+                    func=COPY,
+                    scale=d_t[:, kc, j : j + 1],
+                )
+            else:
+                nc.gpsimd.tensor_scalar(
+                    out=z_t[kc][:, :, j, :],
+                    in0=xh_t[b][:, kc, :, :],
+                    scalar1=d_t[:, kc, j : j + 1],
+                    scalar2=0.0,
+                    op0=MULT,
+                    op1=ADD,
+                )
+
+        def turn(b, g, half):
+            key = (b, g)
+            if half == 0:
+                z_tile = z_pool.tile([P, M, PACK], BF16, align_bytes=64, name="z_turned", bufs=ROUND)
+                z_bf[key] = z_tile
+            zT_ps = tr_psum.tile([P, 2, 2, P], F32, tag="tr")
+            for cc in range(2):
+                words = (
+                    z_t[2 * half + cc][:]
+                    .rearrange("k r j q -> k (r j q)")
+                    .bitcast(F32)
+                    .rearrange("k (p w) -> k p w", p=P)
+                )
+                for u in range(2):
+                    nc.tensor.transpose(zT_ps[:, u, cc, :], words[:, :, 2 * g + u], ident_f32[:])
+            nc.scalar.copy(
+                out=z_bf[key][:, half * 2 * P : (half + 1) * 2 * P, :].bitcast(F32),
+                in_=zT_ps[:].rearrange("p u c k -> p (c k) u"),
+            )
+
+        def regroup_weights_turned(h):
+            flat = w_sb[h][:].rearrange("o i j -> o (i j)")
+            grouped = work.tile([P, W_PASSES, CO, PACK], BF16, align_bytes=64, name="w_grouped")
+            for half in range(W_PASSES // 2):
+                wT_ps = tr_psum.tile([P, 2, PACK, CO], BF16, tag="tr")
+                for gg in range(2):
+                    for t in range(PACK):
+                        c0 = (2 * half + gg) * K_PASS + t * P
+                        nc.tensor.transpose(wT_ps[:, gg, t, :], flat[:, c0 : c0 + P], ident_bf[:])
+                nc.scalar.copy(
+                    out=grouped[:, 2 * half : 2 * half + 2, :, :],
+                    in_=wT_ps[:].rearrange("p g t o -> p g o t"),
+                )
+            w_grouped[h] = grouped
+
+        for_vector = {}
+
+        def later(r, job):
+            for_vector.setdefault(r, []).append(job)
 
         def regroup_for(passes):
             for s in passes:
                 b, it, gl = where(s)
                 if b == 0 and gl % W_PASSES == 0:
-                    h = (it * TILE_PASSES + gl) // W_PASSES
-                    regroup_weights(h)
-                    if h + W_BUFS < W_LOADS:
-                        load_weights(h + W_BUFS)
-                    if h + W_BUFS == W_LOADS - 1:
-                        load_bases(0)
-                        load_bases(1)
-                if it == CH_TILES - 2 and gl == 0:
-                    regroup_bases(b)
-
-        def is_last(s):
-            b, it, gl = where(s)
-            return it == CH_TILES - 1 and gl == TILE_PASSES - 1
+                    regroup_weights((it * TILE_PASSES + gl) // W_PASSES)
+                    load_next_weights()
 
         def quantise_for(passes):
             for s in passes:
                 b, it, gl = where(s)
                 if b == 0 and gl % W_PASSES == 0:
                     quantise_weights((it * TILE_PASSES + gl) // W_PASSES)
-                if it == CH_TILES - 2 and gl == ROUND:
-                    quantise_bases(b)
 
-        project(0)
+        def turned_weights(h, r):
+            regroup_weights_turned(h)
+            load_next_weights()
+            later(r + 1, lambda: quantise_weights(h))
+
+        def turned_bases(b, half, r):
+            regroup_bases(b, half)
+            later(r + 1, lambda: quantise_bases(b, half))
+
+        all_chunks = list(range(M_CHUNKS))
+        prepare(0)
+        project(0, all_chunks)
+        replicate(0)
         for s in gpsimd_first(passes_of(0)):
             widen(s)
-        project(1)
+        transpose_x(0, TURNED_TILE, "xT_turned")
+        replicate(1)
+        transpose_d()
+        project_turned(0)
+        load_bases(0, 2)
+        load_bases(0, 3)
 
-        rounds = (ALL_PASSES + ROUND - 1) // ROUND
-        for r in range(rounds + 2):
-            for s in gpsimd_first(passes_of(r + 1)):
-                widen(s)
-            project(r + 2)
+        now = [0]
+        for_gpsimd = []
+        turned_ready = []
+
+        def job_multiply(b, kc, j):
+            def run():
+                if j == 0:
+                    for jj in range(KM - ON_GPSIMD, KM):
+                        for_gpsimd.append((b, kc, jj))
+                multiply_turned(True, b, kc, j)
+            return run
+
+        def job_turn(b, g, half):
+            def run():
+                turn(b, g, half)
+                if half == 1:
+                    turned_ready.append((b, g))
+            return run
+
+        chain = []
+        for b in range(B):
+            for kc in range(M_CHUNKS):
+                for j in range(KM - ON_GPSIMD):
+                    chain.append((P, job_multiply(b, kc, j)))
+                if b == 0 and kc >= 2:
+                    h = 4 + kc
+                    chain.append((4 * M, lambda h=h: turned_weights(h, now[0])))
+            for g in range(TILE_PASSES):
+                for half in range(2):
+                    chain.append((M, job_turn(b, g, half)))
+                if g % ROUND == ROUND - 1:
+                    half = g // ROUND
+                    chain.append((2 * M, lambda b=b, half=half: turned_bases(b, half, now[0])))
+        owed = [0]
+        at = [0]
+
+        def turned_work(columns):
+            owed[0] = owed[0] + columns
+            while at[0] < len(chain) and owed[0] > 0:
+                cost, job = chain[at[0]]
+                at[0] = at[0] + 1
+                owed[0] = owed[0] - cost
+                job()
+
+        rounds = WIDE_PASSES // ROUND
+        for r in range(rounds + 3):
+            now[0] = r
+            nxt = gpsimd_first(passes_of(r + 1))
+            fresh = []
+            prepare(r + 2)
+            if r == 1:
+                transpose_x(1, TURNED_TILE, "xT_turned")
+            if r == 5:
+                for pair in range(4):
+                    load_bases(1, pair)
+            for n in range(ROUND):
+                if n < len(nxt):
+                    widen(nxt[n])
+                project(r + 2, [n])
+                turned_work(SLOT_COLUMNS)
+                if n == ROUND - 2:
+                    fresh.extend(turned_ready)
+                    turned_ready.clear()
+            replicate(r + 2)
+            if r == 1:
+                project_turned(1)
             for s in gpsimd_first(passes_of(r)):
                 multiply(s)
-            quantise_for(passes_of(r - 1))
-            for s in passes_of(r - 2):
-                if is_last(s):
-                    quantise_y_hat(where(s)[0])
+                if on_gpsimd(s):
+                    for b, kc, j in for_gpsimd:
+                        multiply_turned(False, b, kc, j)
+                    for_gpsimd.clear()
+            quantise_for(passes_of(r) if r > 1 else passes_of(0) + passes_of(1) if r == 1 else [])
+            for job in for_vector.get(r, []):
+                job()
+            for b in range(B):
+                if finished.get(b) == r - 1:
+                    quantise_y_hat(b)
             for s in passes_of(r):
-                quantise(s)
+                if not on_gpsimd(s):
+                    quantise(s)
+            for key in fresh:
+                quantise(key)
+            for s in passes_of(r):
+                if on_gpsimd(s):
+                    quantise(s)
+            regroup_for(passes_of(r + 1) if r > 0 else passes_of(0) + passes_of(1))
             for s in passes_of(r - 1):
-                contract(s)
-                if is_last(s):
-                    regroup_y_hat(where(s)[0])
-            for s in passes_of(r - 2):
-                if is_last(s):
-                    reconstruct(where(s)[0])
-            regroup_for(passes_of(r))
+                b, it, gl = where(s)
+                contract(s, b, it * TILE_PASSES + gl, r)
+            for key in fresh:
+                contract(key, key[0], TURNED_TILE * TILE_PASSES + key[1], r)
+            for b in range(B):
+                if finished.get(b) == r - 1:
+                    reconstruct(b)

@@ -34,9 +34,11 @@ WIDE_TILES = 3
 TURNED_TILE = WIDE_TILES
 WIDE_PASSES = B * WIDE_TILES * TILE_PASSES
 CLASSES = 4
-QUADS = P // CLASSES
+PAIRS = TILE_PASSES // 2
+LINE = 8
 TURN_ROUNDS = TILE_PASSES // ROUND
-SLOT_COLUMNS = 1024
+SLOT_COLUMNS = 1344
+TURNED_PREP = 3
 ON_GPSIMD = 6
 
 FLOPS = 2 * B * (CI * N * M + CI * KM * CO * M + CO * M * N)
@@ -149,6 +151,10 @@ def tile_phydgalerkinconv_k_kernel(tc, x, wbases, bases, weights, D, out):
         y_mx = {}
         acc = {}
         done = {0: 0, 1: 0}
+        owed = [0]
+
+        def pay(columns):
+            owed[0] = owed[0] - columns
         finished = {}
 
         def on_gpsimd(s):
@@ -180,6 +186,7 @@ def tile_phydgalerkinconv_k_kernel(tc, x, wbases, bases, weights, D, out):
             if starts_tile(r):
                 b, it, gl = where(r * ROUND)
                 transpose_x(b, it, "xT_sb")
+                pay(M)
 
         def project(r, chunks):
             if not starts_tile(r):
@@ -356,7 +363,10 @@ def tile_phydgalerkinconv_k_kernel(tc, x, wbases, bases, weights, D, out):
                     stop=True,
                 )
                 o_sb = work.tile([P, N_HALF], F32, name="f32_row")
-                nc.scalar.copy(out=o_sb[:], in_=o_ps[:])
+                if half == 0 or b == 0:
+                    nc.scalar.copy(out=o_sb[:], in_=o_ps[:])
+                else:
+                    nc.vector.tensor_copy(out=o_sb[:], in_=o_ps[:])
                 nc.sync.dma_start(out=out[b, :, cols], in_=o_sb[:])
 
         def transpose_d():
@@ -382,25 +392,30 @@ def tile_phydgalerkinconv_k_kernel(tc, x, wbases, bases, weights, D, out):
                         start=(c == 0),
                         stop=(c == N_CHUNKS - 1),
                     )
-            xh_tile = work.tile([P, M_CHUNKS, CLASSES, QUADS], F32, name="xh_turned")
-            nc.scalar.copy(out=xh_tile[:], in_=xh_ps[:].rearrange("k c (q r) -> k c r q", r=CLASSES))
+            xh_tile = work.tile([P, M_CHUNKS * PAIRS, CLASSES, 2, 2, 2], F32, name="xh_turned")
+            source = xh_ps[:].rearrange("k c (y a m e r) -> k (c y) a m r e", y=PAIRS, a=2, m=2, e=2)
+            for a in range(2):
+                for m in range(2):
+                    nc.scalar.copy(out=xh_tile[:, :, :, m, a, :], in_=source[:, :, a, m, :, :])
             xh_t[b] = xh_tile
 
         def multiply_turned(on_scalar, b, kc, j):
             if j == 0:
-                z_tile = keep.tile([P, CLASSES, KM, QUADS], BF16, name="z_t%d" % kc)
+                z_tile = keep.tile([P, 2, PAIRS, CLASSES, KM // 2, LINE], BF16, name="z_t%d" % kc)
                 z_t[kc] = z_tile
+            product = z_t[kc][:, j % 2, :, :, j // 2, :]
+            factor = xh_t[b][:, kc * PAIRS : (kc + 1) * PAIRS, :, :, :, :].rearrange("k y r m a e -> k y r (m a e)")
             if on_scalar:
                 nc.scalar.activation(
-                    out=z_t[kc][:, :, j, :],
-                    in_=xh_t[b][:, kc, :, :],
+                    out=product,
+                    in_=factor,
                     func=COPY,
                     scale=d_t[:, kc, j : j + 1],
                 )
             else:
                 nc.gpsimd.tensor_scalar(
-                    out=z_t[kc][:, :, j, :],
-                    in0=xh_t[b][:, kc, :, :],
+                    out=product,
+                    in0=factor,
                     scalar1=d_t[:, kc, j : j + 1],
                     scalar2=0.0,
                     op0=MULT,
@@ -416,26 +431,35 @@ def tile_phydgalerkinconv_k_kernel(tc, x, wbases, bases, weights, D, out):
             for cc in range(2):
                 words = (
                     z_t[2 * half + cc][:]
-                    .rearrange("k r j q -> k (r j q)")
+                    .rearrange("k u y r q l -> k (u y r q l)")
                     .bitcast(F32)
-                    .rearrange("k (p w) -> k p w", p=P)
+                    .rearrange("k (u y w) -> k u y w", u=2, y=PAIRS)
                 )
                 for u in range(2):
-                    nc.tensor.transpose(zT_ps[:, u, cc, :], words[:, :, 2 * g + u], ident_f32[:])
+                    nc.tensor.transpose(zT_ps[:, u, cc, :], words[:, u, g // 2, g % 2 : 2 * P : 2], ident_f32[:])
             nc.scalar.copy(
                 out=z_bf[key][:, half * 2 * P : (half + 1) * 2 * P, :].bitcast(F32),
                 in_=zT_ps[:].rearrange("p u c k -> p (c k) u"),
             )
 
         def regroup_weights_turned(h):
-            flat = w_sb[h][:].rearrange("o i j -> o (i j)")
+            source = w_sb[h][:].rearrange("o i j -> o (i j)").rearrange(
+                "o (g m e q u) -> o g u e q m", g=W_PASSES, m=2, e=2, u=2
+            )
+            w_perm = work.tile([P, W_PASSES, 2, 2, P // 2, 2], BF16, align_bytes=64, name="b_grouped")
+            for g in range(W_PASSES):
+                for u in range(2):
+                    nc.scalar.copy(out=w_perm[:, g, u, :, :, :], in_=source[:, g, u, :, :, :])
             grouped = work.tile([P, W_PASSES, CO, PACK], BF16, align_bytes=64, name="w_grouped")
             for half in range(W_PASSES // 2):
                 wT_ps = tr_psum.tile([P, 2, PACK, CO], BF16, tag="tr")
                 for gg in range(2):
                     for t in range(PACK):
-                        c0 = (2 * half + gg) * K_PASS + t * P
-                        nc.tensor.transpose(wT_ps[:, gg, t, :], flat[:, c0 : c0 + P], ident_bf[:])
+                        nc.tensor.transpose(
+                            wT_ps[:, gg, t, :],
+                            w_perm[:, 2 * half + gg, t // 2, t % 2, :, :].rearrange("o q m -> o (q m)"),
+                            ident_bf[:],
+                        )
                 nc.scalar.copy(
                     out=grouped[:, 2 * half : 2 * half + 2, :, :],
                     in_=wT_ps[:].rearrange("p g t o -> p g o t"),
@@ -452,6 +476,7 @@ def tile_phydgalerkinconv_k_kernel(tc, x, wbases, bases, weights, D, out):
                 b, it, gl = where(s)
                 if b == 0 and gl % W_PASSES == 0:
                     regroup_weights((it * TILE_PASSES + gl) // W_PASSES)
+                    pay(2 * M)
                     load_next_weights()
 
         def quantise_for(passes):
@@ -494,46 +519,60 @@ def tile_phydgalerkinconv_k_kernel(tc, x, wbases, bases, weights, D, out):
                 multiply_turned(True, b, kc, j)
             return run
 
-        def job_turn(b, g, half):
+        def job_turn(b, g):
             def run():
-                turn(b, g, half)
-                if half == 1:
-                    turned_ready.append((b, g))
+                turn(b, g, 0)
+                turn(b, g, 1)
+                turned_ready.append((b, g))
             return run
 
         chain = []
         for b in range(B):
             for kc in range(M_CHUNKS):
                 for j in range(KM - ON_GPSIMD):
-                    chain.append((P, job_multiply(b, kc, j)))
+                    chain.append((P, job_multiply(b, kc, j), False))
                 if b == 0 and kc >= 2:
                     h = 4 + kc
-                    chain.append((4 * M, lambda h=h: turned_weights(h, now[0])))
+                    chain.append((8 * M, lambda h=h: turned_weights(h, now[0]), False))
             for g in range(TILE_PASSES):
-                for half in range(2):
-                    chain.append((M, job_turn(b, g, half)))
+                chain.append((2 * M, job_turn(b, g), True))
                 if g % ROUND == ROUND - 1:
                     half = g // ROUND
-                    chain.append((2 * M, lambda b=b, half=half: turned_bases(b, half, now[0])))
-        owed = [0]
+                    chain.append((2 * M, lambda b=b, half=half: turned_bases(b, half, now[0]), False))
         at = [0]
 
         def turned_work(columns):
             owed[0] = owed[0] + columns
+            turned = 0
             while at[0] < len(chain) and owed[0] > 0:
-                cost, job = chain[at[0]]
+                cost, job, is_pass = chain[at[0]]
+                if is_pass and (turned == 1 or for_gpsimd):
+                    return
+                turned = turned + (1 if is_pass else 0)
                 at[0] = at[0] + 1
                 owed[0] = owed[0] - cost
                 job()
 
         rounds = WIDE_PASSES // ROUND
-        for r in range(rounds + 3):
+        fresh = []
+        midway = []
+        at_end = []
+        for r in range(rounds + 5):
             now[0] = r
             nxt = gpsimd_first(passes_of(r + 1))
-            fresh = []
+            for s in passes_of(r - 1) if r > 2 else passes_of(0) + passes_of(1) if r == 2 else []:
+                b, it, gl = where(s)
+                contract(s, b, it * TILE_PASSES + gl, r)
+            for key in fresh:
+                contract(key, key[0], TURNED_TILE * TILE_PASSES + key[1], r)
+            fresh.clear()
+            for b in range(B):
+                if finished.get(b) == r - 1:
+                    reconstruct(b)
             prepare(r + 2)
-            if r == 1:
+            if r == TURNED_PREP:
                 transpose_x(1, TURNED_TILE, "xT_turned")
+                pay(M)
             if r == 5:
                 for pair in range(4):
                     load_bases(1, pair)
@@ -542,38 +581,44 @@ def tile_phydgalerkinconv_k_kernel(tc, x, wbases, bases, weights, D, out):
                     widen(nxt[n])
                 project(r + 2, [n])
                 turned_work(SLOT_COLUMNS)
-                if n == ROUND - 2:
-                    fresh.extend(turned_ready)
+                if n == ROUND // 2 - 1:
+                    at_end.extend(turned_ready)
                     turned_ready.clear()
             replicate(r + 2)
-            if r == 1:
+            regroup_for(passes_of(r + 1) if r > 0 else passes_of(0) + passes_of(1))
+            if r == TURNED_PREP:
                 project_turned(1)
-            for s in gpsimd_first(passes_of(r)):
+                pay(M)
+            for n, s in enumerate(gpsimd_first(passes_of(r))):
                 multiply(s)
                 if on_gpsimd(s):
                     for b, kc, j in for_gpsimd:
                         multiply_turned(False, b, kc, j)
                     for_gpsimd.clear()
-            quantise_for(passes_of(r) if r > 1 else passes_of(0) + passes_of(1) if r == 1 else [])
+                if n == ROUND - 2:
+                    for key in midway:
+                        quantise(key)
+                    fresh.extend(midway)
+                    midway.clear()
+            for key in midway:
+                quantise(key)
+            fresh.extend(midway)
+            midway.clear()
             for job in for_vector.get(r, []):
                 job()
             for b in range(B):
-                if finished.get(b) == r - 1:
+                if finished.get(b) == r:
                     quantise_y_hat(b)
             for s in passes_of(r):
                 if not on_gpsimd(s):
                     quantise(s)
-            for key in fresh:
+            quantise_for(passes_of(r) if r > 1 else passes_of(0) + passes_of(1) if r == 1 else [])
+            for key in at_end:
                 quantise(key)
+            fresh.extend(at_end)
+            at_end.clear()
             for s in passes_of(r):
                 if on_gpsimd(s):
                     quantise(s)
-            regroup_for(passes_of(r + 1) if r > 0 else passes_of(0) + passes_of(1))
-            for s in passes_of(r - 1):
-                b, it, gl = where(s)
-                contract(s, b, it * TILE_PASSES + gl, r)
-            for key in fresh:
-                contract(key, key[0], TURNED_TILE * TILE_PASSES + key[1], r)
-            for b in range(B):
-                if finished.get(b) == r - 1:
-                    reconstruct(b)
+            midway.extend(turned_ready)
+            turned_ready.clear()

@@ -39,7 +39,8 @@ LINE = 8
 TURN_ROUNDS = TILE_PASSES // ROUND
 SLOT_COLUMNS = 1344
 TURNED_PREP = 3
-ON_GPSIMD = 6
+GPSIMD_A_ROUND = 4
+ON_GPSIMD = 8
 
 FLOPS = 2 * B * (CI * N * M + CI * KM * CO * M + CO * M * N)
 
@@ -136,7 +137,7 @@ def tile_phydgalerkinconv_k_kernel(tc, x, wbases, bases, weights, D, out):
         b_scales = [keep.tile([P, N], U8, align_bytes=64, name="b_scales%d" % b) for b in range(B)]
 
         d_t = const.tile([P, M_CHUNKS, KM], F32)
-        xh_t = {}
+        xh_t = keep.tile([P, M_CHUNKS * PAIRS, B, CLASSES, 2, 2, 2], F32)
         z_t = {}
 
         x_t = {}
@@ -146,8 +147,11 @@ def tile_phydgalerkinconv_k_kernel(tc, x, wbases, bases, weights, D, out):
         z_bf = {}
         z_mx = {}
         w_grouped = {}
+        w_permuted = {}
         b_grouped = {}
         y_grouped = {}
+        y_rows = {}
+        closed = []
         y_mx = {}
         acc = {}
         done = {0: 0, 1: 0}
@@ -248,12 +252,12 @@ def tile_phydgalerkinconv_k_kernel(tc, x, wbases, bases, weights, D, out):
 
         def quantise(s):
             turned = s not in wide
-            z_codes = z_pool.tile([P, M], U32, align_bytes=64, name="zt_codes" if turned else "z_codes", bufs=ROUND if turned else 2 * ROUND)
-            z_scales = z_pool.tile([P, M], U8, align_bytes=64, name="zt_scales" if turned else "z_scales", bufs=ROUND if turned else 2 * ROUND)
+            z_codes = z_pool.tile([P, M], U32, align_bytes=64, name="zt_codes" if turned else "z_codes", bufs=3 if turned else 2 * ROUND + 1)
+            z_scales = z_pool.tile([P, M], U8, align_bytes=64, name="zt_scales" if turned else "z_scales", bufs=3 if turned else 2 * ROUND + 1)
             nc.vector.quantize_mx(
                 out=z_codes[:].bitcast(FP8X4),
                 scales=z_scales[:],
-                in_=z_bf[s][:].rearrange("p k t -> p (k t)"),
+                in_=z_bf[s][:].rearrange("p b a k t -> p (b a k t)") if turned else z_bf[s][:].rearrange("p k t -> p (k t)"),
             )
             z_mx[s] = (z_codes, z_scales)
 
@@ -269,11 +273,11 @@ def tile_phydgalerkinconv_k_kernel(tc, x, wbases, bases, weights, D, out):
                 rhs=z_codes[:].bitcast(FP8X4),
                 rhs_scale=z_scales[:],
                 start=(done[b] == 0),
-                stop=(done[b] == PASSES - 1),
+                stop=(done[b] == WIDE_TILES * TILE_PASSES - 1),
             )
             done[b] = done[b] + 1
-            if done[b] == PASSES:
-                regroup_y_hat(b)
+            if done[b] == WIDE_TILES * TILE_PASSES:
+                closed.append(b)
                 finished[b] = r
 
         def regroup_weights(h):
@@ -327,10 +331,13 @@ def tile_phydgalerkinconv_k_kernel(tc, x, wbases, bases, weights, D, out):
                 in_=b_grouped[(b, half)][:].rearrange("p c n t -> p (c n t)"),
             )
 
-        def regroup_y_hat(b):
-            y_sb = work.tile([P, M], F32, name="f32_row")
+        def fetch_y_hat(b):
+            y_sb = work.tile([P, M], F32, name="f32_row", bufs=4)
             nc.scalar.copy(out=y_sb[:], in_=acc[b][:])
-            y_cols = y_sb[:].rearrange("o (p t) -> o t p", t=PACK)
+            y_rows[b] = y_sb
+
+        def regroup_y_hat(b):
+            y_cols = y_rows[b][:].rearrange("o (p t) -> o t p", t=PACK)
             yT_ps = tr_psum.tile([P, PACK, CO], F32, tag="tr")
             for t in range(PACK):
                 nc.tensor.transpose(yT_ps[:, t, :], y_cols[:, t, :], ident_f32[:])
@@ -362,7 +369,7 @@ def tile_phydgalerkinconv_k_kernel(tc, x, wbases, bases, weights, D, out):
                     start=True,
                     stop=True,
                 )
-                o_sb = work.tile([P, N_HALF], F32, name="f32_row")
+                o_sb = work.tile([P, N_HALF], F32, name="f32_row", bufs=4)
                 if half == 0 or b == 0:
                     nc.scalar.copy(out=o_sb[:], in_=o_ps[:])
                 else:
@@ -382,7 +389,7 @@ def tile_phydgalerkinconv_k_kernel(tc, x, wbases, bases, weights, D, out):
                 )
 
         def project_turned(b):
-            xh_ps = xh_psum.tile([P, M_CHUNKS, P], F32)
+            xh_ps = tr_psum.tile([P, M_CHUNKS, P], F32, tag="tr")
             for kc in range(M_CHUNKS):
                 for c in range(N_CHUNKS):
                     nc.tensor.matmul(
@@ -392,19 +399,22 @@ def tile_phydgalerkinconv_k_kernel(tc, x, wbases, bases, weights, D, out):
                         start=(c == 0),
                         stop=(c == N_CHUNKS - 1),
                     )
-            xh_tile = work.tile([P, M_CHUNKS * PAIRS, CLASSES, 2, 2, 2], F32, name="xh_turned")
             source = xh_ps[:].rearrange("k c (y a m e r) -> k (c y) a m r e", y=PAIRS, a=2, m=2, e=2)
             for a in range(2):
                 for m in range(2):
-                    nc.scalar.copy(out=xh_tile[:, :, :, m, a, :], in_=source[:, :, a, m, :, :])
-            xh_t[b] = xh_tile
+                    nc.scalar.copy(out=xh_t[:, :, b, :, m, a, :], in_=source[:, :, a, m, :, :])
 
         def multiply_turned(on_scalar, b, kc, j):
-            if j == 0:
-                z_tile = keep.tile([P, 2, PAIRS, CLASSES, KM // 2, LINE], BF16, name="z_t%d" % kc)
+            if kc not in z_t:
+                z_tile = keep.tile([P, 2, PAIRS, B, CLASSES, KM // 2, LINE], BF16, name="z_t", bufs=2)
                 z_t[kc] = z_tile
-            product = z_t[kc][:, j % 2, :, :, j // 2, :]
-            factor = xh_t[b][:, kc * PAIRS : (kc + 1) * PAIRS, :, :, :, :].rearrange("k y r m a e -> k y r (m a e)")
+            pairs = slice(kc * PAIRS, (kc + 1) * PAIRS)
+            if b is None:
+                product = z_t[kc][:, j % 2, :, :, :, j // 2, :].rearrange("k y b r l -> k (y b r) l")
+                factor = xh_t[:, pairs, :, :, :, :, :].rearrange("k y b r m a e -> k (y b r) (m a e)")
+            else:
+                product = z_t[kc][:, j % 2, :, b, :, j // 2, :]
+                factor = xh_t[:, pairs, b, :, :, :, :].rearrange("k y r m a e -> k y r (m a e)")
             if on_scalar:
                 nc.scalar.activation(
                     out=product,
@@ -422,27 +432,42 @@ def tile_phydgalerkinconv_k_kernel(tc, x, wbases, bases, weights, D, out):
                     op1=ADD,
                 )
 
-        def turn(b, g, half):
-            key = (b, g)
-            if half == 0:
-                z_tile = z_pool.tile([P, M, PACK], BF16, align_bytes=64, name="z_turned", bufs=ROUND)
-                z_bf[key] = z_tile
-            zT_ps = tr_psum.tile([P, 2, 2, P], F32, tag="tr")
-            for cc in range(2):
-                words = (
-                    z_t[2 * half + cc][:]
-                    .rearrange("k u y r q l -> k (u y r q l)")
-                    .bitcast(F32)
-                    .rearrange("k (u y w) -> k u y w", u=2, y=PAIRS)
-                )
-                for u in range(2):
-                    nc.tensor.transpose(zT_ps[:, u, cc, :], words[:, u, g // 2, g % 2 : 2 * P : 2], ident_f32[:])
-            nc.scalar.copy(
-                out=z_bf[key][:, half * 2 * P : (half + 1) * 2 * P, :].bitcast(F32),
-                in_=zT_ps[:].rearrange("p u c k -> p (c k) u"),
+        def turn(kc, y):
+            z_tile = z_pool.tile([P, B, 2, P, PACK], BF16, align_bytes=64, name="z_turned", bufs=3)
+            words = (
+                z_t[kc][:]
+                .rearrange("k u y b r q l -> k (u y b r q l)")
+                .bitcast(F32)
+                .rearrange("k (u y b w) -> k u y b w", u=2, y=PAIRS, b=B)
             )
+            for b in range(B):
+                zT_ps = tr_psum.tile([P, 2, 2, P], F32, tag="tr")
+                for u in range(2):
+                    for a in range(2):
+                        nc.tensor.transpose(zT_ps[:, u, a, :], words[:, u, y, b, a : 2 * P : 2], ident_f32[:])
+                nc.scalar.copy(
+                    out=z_tile[:, b, :, :, :].bitcast(F32),
+                    in_=zT_ps[:].rearrange("p u a k -> p a k u"),
+                )
+            z_bf[(kc, y)] = z_tile
 
-        def regroup_weights_turned(h):
+        def contract_turned(kc, y):
+            z_codes, z_scales = z_mx[(kc, y)]
+            for b in range(B):
+                for a in range(2):
+                    g = TURNED_TILE * TILE_PASSES + 2 * y + a
+                    cols = slice((2 * b + a) * P, (2 * b + a + 1) * P)
+                    nc.tensor.matmul_mx(
+                        out=acc[b][:, kc * P : (kc + 1) * P],
+                        lhsT=w_codes[:, g, :].bitcast(FP8X4),
+                        lhsT_scale=w_scales[:, g, :],
+                        rhs=z_codes[:, cols].bitcast(FP8X4),
+                        rhs_scale=z_scales[:, cols],
+                        start=False,
+                        stop=False,
+                    )
+
+        def permute_weights_turned(h):
             source = w_sb[h][:].rearrange("o i j -> o (i j)").rearrange(
                 "o (g m e q u) -> o g u e q m", g=W_PASSES, m=2, e=2, u=2
             )
@@ -450,6 +475,11 @@ def tile_phydgalerkinconv_k_kernel(tc, x, wbases, bases, weights, D, out):
             for g in range(W_PASSES):
                 for u in range(2):
                     nc.scalar.copy(out=w_perm[:, g, u, :, :, :], in_=source[:, g, u, :, :, :])
+            w_permuted[h] = w_perm
+            load_next_weights()
+
+        def regroup_weights_turned(h):
+            w_perm = w_permuted[h]
             grouped = work.tile([P, W_PASSES, CO, PACK], BF16, align_bytes=64, name="w_grouped")
             for half in range(W_PASSES // 2):
                 wT_ps = tr_psum.tile([P, 2, PACK, CO], BF16, tag="tr")
@@ -467,6 +497,7 @@ def tile_phydgalerkinconv_k_kernel(tc, x, wbases, bases, weights, D, out):
             w_grouped[h] = grouped
 
         for_vector = {}
+        weights_round = [0]
 
         def later(r, job):
             for_vector.setdefault(r, []).append(job)
@@ -487,8 +518,8 @@ def tile_phydgalerkinconv_k_kernel(tc, x, wbases, bases, weights, D, out):
 
         def turned_weights(h, r):
             regroup_weights_turned(h)
-            load_next_weights()
             later(r + 1, lambda: quantise_weights(h))
+            weights_round[0] = r
 
         def turned_bases(b, half, r):
             regroup_bases(b, half)
@@ -513,40 +544,52 @@ def tile_phydgalerkinconv_k_kernel(tc, x, wbases, bases, weights, D, out):
 
         def job_multiply(b, kc, j):
             def run():
-                if j == 0:
+                if j == 0 and b != 0:
                     for jj in range(KM - ON_GPSIMD, KM):
-                        for_gpsimd.append((b, kc, jj))
+                        for_gpsimd.append((kc, jj))
                 multiply_turned(True, b, kc, j)
             return run
 
-        def job_turn(b, g):
+        def job_turn(kc, y):
             def run():
-                turn(b, g, 0)
-                turn(b, g, 1)
-                turned_ready.append((b, g))
+                turn(kc, y)
+                turned_ready.append((kc, y))
             return run
 
-        chain = []
-        for b in range(B):
-            for kc in range(M_CHUNKS):
+        products = {}
+        for kc in range(M_CHUNKS):
+            products[kc] = []
+            for b in range(B) if kc == 0 else [None]:
                 for j in range(KM - ON_GPSIMD):
-                    chain.append((P, job_multiply(b, kc, j), False))
-                if b == 0 and kc >= 2:
-                    h = 4 + kc
-                    chain.append((8 * M, lambda h=h: turned_weights(h, now[0]), False))
-            for g in range(TILE_PASSES):
-                chain.append((2 * M, job_turn(b, g), True))
-                if g % ROUND == ROUND - 1:
-                    half = g // ROUND
-                    chain.append((2 * M, lambda b=b, half=half: turned_bases(b, half, now[0]), False))
+                    products[kc].append((P if kc == 0 else 2 * P, job_multiply(b, kc, j), 2 if b == 1 else 0))
+                    if b == 1 and j in (2, 8, 14, 20):
+                        h = 6 + j // 12
+                        if j % 12 == 2:
+                            products[kc].append((4 * M, lambda h=h: permute_weights_turned(h), 0))
+                        else:
+                            products[kc].append((4 * M, lambda h=h: turned_weights(h, now[0]), 0))
+        products[M_CHUNKS] = []
+        chain = list(products[0])
+        for kc in range(M_CHUNKS):
+            count = len(products[kc + 1])
+            for y in range(PAIRS):
+                chain.append((2 * M, job_turn(kc, y), -1 - kc))
+                chain.extend(products[kc + 1][y * count // PAIRS : (y + 1) * count // PAIRS])
+                if kc in (1, 2) and y % 2 == 1:
+                    chain.append((2 * M, lambda b=kc - 1, half=y // 2: turned_bases(b, half, now[0]), 0))
         at = [0]
 
         def turned_work(columns):
             owed[0] = owed[0] + columns
             turned = 0
             while at[0] < len(chain) and owed[0] > 0:
-                cost, job, is_pass = chain[at[0]]
-                if is_pass and (turned == 1 or for_gpsimd):
+                cost, job, kind = chain[at[0]]
+                is_pass = kind < 0
+                if is_pass and (turned == 1 or any(kc <= -1 - kind for kc, j in for_gpsimd)):
+                    return
+                if is_pass and now[0] <= weights_round[0]:
+                    return
+                if not is_pass and kind > now[0]:
                     return
                 turned = turned + (1 if is_pass else 0)
                 at[0] = at[0] + 1
@@ -555,22 +598,36 @@ def tile_phydgalerkinconv_k_kernel(tc, x, wbases, bases, weights, D, out):
 
         rounds = WIDE_PASSES // ROUND
         fresh = []
-        midway = []
         at_end = []
+        held = []
+        turned_left = [M_CHUNKS * PAIRS]
         for r in range(rounds + 5):
             now[0] = r
             nxt = gpsimd_first(passes_of(r + 1))
-            for s in passes_of(r - 1) if r > 2 else passes_of(0) + passes_of(1) if r == 2 else []:
-                b, it, gl = where(s)
-                contract(s, b, it * TILE_PASSES + gl, r)
             for key in fresh:
-                contract(key, key[0], TURNED_TILE * TILE_PASSES + key[1], r)
+                contract_turned(key[0], key[1])
+                turned_left[0] = turned_left[0] - 1
             fresh.clear()
+            held.extend(passes_of(r - 1) if r > 2 else passes_of(0) + passes_of(1) if r == 2 else [])
+            waiting = []
+            for s in held:
+                b, it, gl = where(s)
+                if it == WIDE_TILES - 1 and gl == TILE_PASSES - 1 and turned_left[0] > 0:
+                    waiting.append(s)
+                else:
+                    contract(s, b, it * TILE_PASSES + gl, r)
+            held.clear()
+            held.extend(waiting)
+            for b in closed:
+                fetch_y_hat(b)
+            for b in closed:
+                regroup_y_hat(b)
+            closed.clear()
             for b in range(B):
                 if finished.get(b) == r - 1:
                     reconstruct(b)
             prepare(r + 2)
-            if r == TURNED_PREP:
+            if r == 1:
                 transpose_x(1, TURNED_TILE, "xT_turned")
                 pay(M)
             if r == 5:
@@ -580,30 +637,27 @@ def tile_phydgalerkinconv_k_kernel(tc, x, wbases, bases, weights, D, out):
                 if n < len(nxt):
                     widen(nxt[n])
                 project(r + 2, [n])
+                if r == 1 and n == 0:
+                    project_turned(1)
+                    pay(M)
                 turned_work(SLOT_COLUMNS)
-                if n == ROUND // 2 - 1:
+                if n == ROUND - 2:
                     at_end.extend(turned_ready)
                     turned_ready.clear()
             replicate(r + 2)
             regroup_for(passes_of(r + 1) if r > 0 else passes_of(0) + passes_of(1))
-            if r == TURNED_PREP:
-                project_turned(1)
-                pay(M)
-            for n, s in enumerate(gpsimd_first(passes_of(r))):
+            for s in gpsimd_first(passes_of(r)):
                 multiply(s)
                 if on_gpsimd(s):
-                    for b, kc, j in for_gpsimd:
-                        multiply_turned(False, b, kc, j)
+                    for kc, j in for_gpsimd[0:GPSIMD_A_ROUND]:
+                        multiply_turned(False, None, kc, j)
+                    rest = for_gpsimd[GPSIMD_A_ROUND:]
                     for_gpsimd.clear()
-                if n == ROUND - 2:
-                    for key in midway:
-                        quantise(key)
-                    fresh.extend(midway)
-                    midway.clear()
-            for key in midway:
-                quantise(key)
-            fresh.extend(midway)
-            midway.clear()
+                    for_gpsimd.extend(rest)
+            if not passes_of(r):
+                for kc, j in for_gpsimd:
+                    multiply_turned(False, None, kc, j)
+                for_gpsimd.clear()
             for job in for_vector.get(r, []):
                 job()
             for b in range(B):
@@ -620,5 +674,4 @@ def tile_phydgalerkinconv_k_kernel(tc, x, wbases, bases, weights, D, out):
             for s in passes_of(r):
                 if on_gpsimd(s):
                     quantise(s)
-            midway.extend(turned_ready)
-            turned_ready.clear()
+        assert at[0] == len(chain) and not held and not for_gpsimd and len(y_mx) == B

@@ -37,7 +37,7 @@ CLASSES = 4
 PAIRS = TILE_PASSES // 2
 LINE = 8
 TURN_ROUNDS = TILE_PASSES // ROUND
-SLOT_COLUMNS = 1344
+SLOT_COLUMNS = 1472
 TURNED_PREP = 3
 GPSIMD_A_ROUND = 4
 ON_GPSIMD = 8
@@ -155,6 +155,7 @@ def tile_phydgalerkinconv_k_kernel(tc, x, wbases, bases, weights, D, out):
         y_mx = {}
         acc = {}
         done = {0: 0, 1: 0}
+        now = [0]
         owed = [0]
 
         def pay(columns):
@@ -192,6 +193,20 @@ def tile_phydgalerkinconv_k_kernel(tc, x, wbases, bases, weights, D, out):
                 transpose_x(b, it, "xT_sb")
                 pay(M)
 
+        def project_half(half):
+            if half == 0:
+                xh_ps = xh_psum.tile([P, M_CHUNKS, TILE_PASSES, CH_PASS], F32)
+                xh[(0, 0)] = xh_ps
+            for kc in range(M_CHUNKS):
+                for c in range(N_CHUNKS):
+                    nc.tensor.matmul(
+                        xh[(0, 0)][:, kc, half * ROUND : (half + 1) * ROUND, :].rearrange("p g i -> p (g i)"),
+                        lhsT=wb_sb[0][:, c, kc * P : (kc + 1) * P],
+                        rhs=x_t[(0, 0)][:, c, half * ROUND * CH_PASS : (half + 1) * ROUND * CH_PASS],
+                        start=(c == 0),
+                        stop=(c == N_CHUNKS - 1),
+                    )
+
         def project(r, chunks):
             if not starts_tile(r):
                 return
@@ -210,7 +225,7 @@ def tile_phydgalerkinconv_k_kernel(tc, x, wbases, bases, weights, D, out):
                     )
 
         def replicate(r):
-            for s in gpsimd_first(passes_of(r)):
+            for s in gpsimd_first(passes_of(r)) if r > 0 else first_order:
                 b, it, gl = where(s)
                 rep_tile = wide_pool.tile([P, M_CHUNKS, CH_PASS, REP], F32, name="x_rep")
                 nc.scalar.copy(
@@ -331,9 +346,15 @@ def tile_phydgalerkinconv_k_kernel(tc, x, wbases, bases, weights, D, out):
                 in_=b_grouped[(b, half)][:].rearrange("p c n t -> p (c n t)"),
             )
 
+        def vector_is_free():
+            return not passes_of(now[0])
+
         def fetch_y_hat(b):
             y_sb = work.tile([P, M], F32, name="f32_row", bufs=4)
-            nc.scalar.copy(out=y_sb[:], in_=acc[b][:])
+            if vector_is_free() and b == 1:
+                nc.vector.tensor_copy(out=y_sb[:], in_=acc[b][:])
+            else:
+                nc.scalar.copy(out=y_sb[:], in_=acc[b][:])
             y_rows[b] = y_sb
 
         def regroup_y_hat(b):
@@ -342,7 +363,10 @@ def tile_phydgalerkinconv_k_kernel(tc, x, wbases, bases, weights, D, out):
             for t in range(PACK):
                 nc.tensor.transpose(yT_ps[:, t, :], y_cols[:, t, :], ident_f32[:])
             grouped = work.tile([P, CO, PACK], BF16, align_bytes=64, name="y_grouped")
-            nc.scalar.copy(out=grouped[:], in_=yT_ps[:].rearrange("p t o -> p o t"))
+            if vector_is_free() and b == 1:
+                nc.vector.tensor_copy(out=grouped[:], in_=yT_ps[:].rearrange("p t o -> p o t"))
+            else:
+                nc.scalar.copy(out=grouped[:], in_=yT_ps[:].rearrange("p t o -> p o t"))
             y_grouped[b] = grouped
 
         def quantise_y_hat(b):
@@ -370,14 +394,14 @@ def tile_phydgalerkinconv_k_kernel(tc, x, wbases, bases, weights, D, out):
                     stop=True,
                 )
                 o_sb = work.tile([P, N_HALF], F32, name="f32_row", bufs=4)
-                if half == 0 or b == 0:
+                if half == 0 or not vector_is_free():
                     nc.scalar.copy(out=o_sb[:], in_=o_ps[:])
                 else:
                     nc.vector.tensor_copy(out=o_sb[:], in_=o_ps[:])
                 nc.sync.dma_start(out=out[b, :, cols], in_=o_sb[:])
 
-        def transpose_d():
-            for half in range(M_CHUNKS // 2):
+        def transpose_d(halves):
+            for half in halves:
                 dT_ps = tr_psum.tile([P, 2, PACK, P], BF16, tag="tr")
                 for cc in range(2):
                     kc = 2 * half + cc
@@ -388,9 +412,12 @@ def tile_phydgalerkinconv_k_kernel(tc, x, wbases, bases, weights, D, out):
                     in_=dT_ps[:, :, :, 0:REP].rearrange("k c t p -> k c p t"),
                 )
 
-        def project_turned(b):
-            xh_ps = tr_psum.tile([P, M_CHUNKS, P], F32, tag="tr")
-            for kc in range(M_CHUNKS):
+        def project_turned(b, chunks):
+            if chunks[0] == 0:
+                xh_ps = tr_psum.tile([P, M_CHUNKS, P], F32, tag="tr")
+                xh[(b, TURNED_TILE)] = xh_ps
+            xh_ps = xh[(b, TURNED_TILE)]
+            for kc in chunks:
                 for c in range(N_CHUNKS):
                     nc.tensor.matmul(
                         xh_ps[:, kc, :],
@@ -399,6 +426,8 @@ def tile_phydgalerkinconv_k_kernel(tc, x, wbases, bases, weights, D, out):
                         start=(c == 0),
                         stop=(c == N_CHUNKS - 1),
                     )
+            if chunks[-1] != M_CHUNKS - 1:
+                return
             source = xh_ps[:].rearrange("k c (y a m e r) -> k (c y) a m r e", y=PAIRS, a=2, m=2, e=2)
             for a in range(2):
                 for m in range(2):
@@ -526,19 +555,15 @@ def tile_phydgalerkinconv_k_kernel(tc, x, wbases, bases, weights, D, out):
             later(r + 1, lambda: quantise_bases(b, half))
 
         all_chunks = list(range(M_CHUNKS))
+        first_order = [0, ROUND - 1] + list(range(1, ROUND - 1))
         prepare(0)
-        project(0, all_chunks)
+        project_half(0)
         replicate(0)
-        for s in gpsimd_first(passes_of(0)):
+        for s in first_order:
             widen(s)
-        transpose_x(0, TURNED_TILE, "xT_turned")
+        project_half(1)
         replicate(1)
-        transpose_d()
-        project_turned(0)
-        load_bases(0, 2)
-        load_bases(0, 3)
 
-        now = [0]
         for_gpsimd = []
         turned_ready = []
 
@@ -604,20 +629,25 @@ def tile_phydgalerkinconv_k_kernel(tc, x, wbases, bases, weights, D, out):
         for r in range(rounds + 5):
             now[0] = r
             nxt = gpsimd_first(passes_of(r + 1))
+            held.extend(passes_of(r - 1) if r > 2 else passes_of(0) + passes_of(1) if r == 2 else [])
+            last = []
+            for s in held:
+                b, it, gl = where(s)
+                if on_gpsimd(s):
+                    last.append(s)
+                else:
+                    contract(s, b, it * TILE_PASSES + gl, r)
+            held.clear()
             for key in fresh:
                 contract_turned(key[0], key[1])
                 turned_left[0] = turned_left[0] - 1
             fresh.clear()
-            held.extend(passes_of(r - 1) if r > 2 else passes_of(0) + passes_of(1) if r == 2 else [])
-            waiting = []
-            for s in held:
+            for s in last:
                 b, it, gl = where(s)
                 if it == WIDE_TILES - 1 and gl == TILE_PASSES - 1 and turned_left[0] > 0:
-                    waiting.append(s)
+                    held.append(s)
                 else:
                     contract(s, b, it * TILE_PASSES + gl, r)
-            held.clear()
-            held.extend(waiting)
             for b in closed:
                 fetch_y_hat(b)
             for b in closed:
@@ -634,19 +664,37 @@ def tile_phydgalerkinconv_k_kernel(tc, x, wbases, bases, weights, D, out):
                 for pair in range(4):
                     load_bases(1, pair)
             for n in range(ROUND):
+                if r == 0 and n == 0:
+                    transpose_x(0, TURNED_TILE, "xT_turned")
                 if n < len(nxt):
                     widen(nxt[n])
-                project(r + 2, [n])
-                if r == 1 and n == 0:
-                    project_turned(1)
-                    pay(M)
-                turned_work(SLOT_COLUMNS)
-                if n == ROUND - 2:
+                if r > 0:
+                    project(r + 2, [n])
+                if r == 0 and n < 2:
+                    project(2, [2 * n, 2 * n + 1])
+                if r == 0 and n == 1:
+                    replicate(2)
+                if r == 0 and n == 2:
+                    transpose_d([0, 1])
+                if r == 0 and n == 3:
+                    project_turned(0, all_chunks)
+                if r == 1:
+                    project_turned(1, [n])
+                    pay(P)
+                if r > 0:
+                    turned_work(SLOT_COLUMNS)
+                if n == ROUND - 3:
                     at_end.extend(turned_ready)
                     turned_ready.clear()
-            replicate(r + 2)
-            regroup_for(passes_of(r + 1) if r > 0 else passes_of(0) + passes_of(1))
-            for s in gpsimd_first(passes_of(r)):
+            if r == 0:
+                load_bases(0, 2)
+                load_bases(0, 3)
+                regroup_for(passes_of(0) + passes_of(1))
+                turned_work(2 * SLOT_COLUMNS)
+            if r > 0:
+                replicate(r + 2)
+                regroup_for(passes_of(r + 1))
+            for s in gpsimd_first(passes_of(r)) if r > 0 else first_order:
                 multiply(s)
                 if on_gpsimd(s):
                     for kc, j in for_gpsimd[0:GPSIMD_A_ROUND]:

from contextlib import ExitStack

import concourse.mybir as mybir
from concourse.masks import make_identity

BF16 = mybir.dt.bfloat16
F32 = mybir.dt.float32
U32 = mybir.dt.uint32
U8 = mybir.dt.uint8
FP8X4 = mybir.dt.float8_e4m3fn_x4
MULT = mybir.AluOpType.mult
ADD = mybir.AluOpType.add
COPY = mybir.ActivationFunctionType.Copy

B, CI, CO, N, KM, M = 2, 512, 128, 1024, 32, 512

P = 128
PACK = 4
K_PASS = P * PACK
CH_PASS = K_PASS // KM
REP = P // CH_PASS
PASSES = CI // CH_PASS
TILE_PASSES = P // CH_PASS
N_CHUNKS = N // P
M_CHUNKS = M // P
W_PASSES = 4
W_CH = W_PASSES * CH_PASS
W_BUFS = 4
N_HALF = 512
ROUND = 4
WIDE_BANKS = 3

WIDE_TILES = 3
TURNED_TILE = WIDE_TILES
WIDE_PASSES = B * WIDE_TILES * TILE_PASSES
CLASSES = 4
PAIRS = TILE_PASSES // 2
LINE = 8
TURN_ROUNDS = TILE_PASSES // ROUND
SLOT_COLUMNS = 1472
TURNED_PREP = 3
GPSIMD_A_ROUND = 4
ON_GPSIMD = 8

FLOPS = 2 * B * (CI * N * M + CI * KM * CO * M + CO * M * N)


def tile_phydgalerkinconv_k_kernel(tc, x, wbases, bases, weights, D, out):
    nc = tc.nc
    with ExitStack() as ctx:
        ctx.enter_context(tc.manual_schedule())
        const = ctx.enter_context(tc.tile_pool(name="const", bufs=1))
        inputs = ctx.enter_context(tc.tile_pool(name="inputs", bufs=1))
        inbox = ctx.enter_context(tc.tile_pool(name="inbox", bufs=10))
        w_in = ctx.enter_context(tc.tile_pool(name="w_in", bufs=W_BUFS))
        keep = ctx.enter_context(tc.tile_pool(name="keep", bufs=1))
        work = ctx.enter_context(tc.tile_pool(name="work", bufs=2))
        wide_pool = ctx.enter_context(tc.tile_pool(name="wide_pool", bufs=2 * ROUND))
        z_pool = ctx.enter_context(tc.tile_pool(name="z_pool", bufs=2 * ROUND))
        acc_psum = ctx.enter_context(tc.psum_pool(name="acc_psum", bufs=1))
        wide_psum = ctx.enter_context(tc.psum_pool(name="wide_psum", bufs=WIDE_BANKS))
        xh_psum = ctx.enter_context(tc.psum_pool(name="xh_psum", bufs=1))
        tr_psum = ctx.enter_context(tc.psum_pool(name="tr_psum", bufs=2))

        x_sb = {}
        bases_sb = {}
        w_sb = {}
        wb_sb = [inputs.tile([P, N_CHUNKS, M], BF16, name="wb_sb%d" % b) for b in range(B)]

        def load_x(b, it):
            in_tile = inbox.tile([P, N], BF16)
            nc.sync.dma_start(out=in_tile[:], in_=x[b, it * P : (it + 1) * P, :])
            x_sb[(b, it)] = in_tile

        def load_wbases(b):
            nc.sync.dma_start(out=wb_sb[b][:], in_=wbases[b].rearrange("(c p) k -> p c k", p=P))

        def load_weights(h):
            w_tile = w_in.tile([P, W_CH, KM], BF16, name="w_tile")
            nc.sync.dma_start(
                out=w_tile[:],
                in_=weights[h * W_CH : (h + 1) * W_CH, :, :].rearrange("i o j -> o i j"),
            )
            w_sb[h] = w_tile

        def load_bases(b, pair):
            in_tile = inbox.tile([P, 2, M], BF16)
            nc.sync.dma_start(
                out=in_tile[:],
                in_=bases[b, 2 * pair * P : 2 * (pair + 1) * P, :].rearrange("(c p) k -> p c k", p=P),
            )
            bases_sb[(b, pair)] = in_tile

        d_rows = work.tile([P, PACK, M], BF16, align_bytes=64, name="b_grouped")

        w_order = [0, 1, 6, 7, 2, 3, 4, 5]

        load_x(0, 0)
        load_wbases(0)
        for h in range(REP):
            nc.sync.dma_start(
                out=d_rows[h:P:REP, :, :],
                in_=D[h * PACK : (h + 1) * PACK, :].unsqueeze(0).to_broadcast([CH_PASS, PACK, M]),
            )
        load_x(0, TURNED_TILE)
        load_x(1, 0)
        load_wbases(1)
        load_weights(w_order[0])
        load_weights(w_order[1])
        load_x(1, TURNED_TILE)
        load_x(0, 1)
        load_weights(w_order[2])
        load_weights(w_order[3])
        load_x(1, 1)
        load_x(0, 2)
        load_x(1, 2)
        load_bases(0, 0)
        load_bases(0, 1)
        w_loaded = [W_BUFS]

        def load_next_weights():
            if w_loaded[0] < len(w_order):
                load_weights(w_order[w_loaded[0]])
                w_loaded[0] = w_loaded[0] + 1

        ident_bf = const.tile([P, P], BF16)
        make_identity(nc, ident_bf[:])
        ident_f32 = const.tile([P, P], F32)
        make_identity(nc, ident_f32[:])

        d_grouped = const.tile([P, M, PACK], BF16)
        nc.vector.tensor_copy(out=d_grouped[:], in_=d_rows[:].rearrange("p t k -> p k t"))

        w_codes = keep.tile([P, PASSES, CO], U32, align_bytes=64)
        w_scales = keep.tile([P, PASSES, CO], U8, align_bytes=64)
        b_codes = [keep.tile([P, N], U32, align_bytes=64, name="b_codes%d" % b) for b in range(B)]
        b_scales = [keep.tile([P, N], U8, align_bytes=64, name="b_scales%d" % b) for b in range(B)]

        d_t = const.tile([P, M_CHUNKS, KM], F32)
        xh_t = keep.tile([P, M_CHUNKS * PAIRS, B, CLASSES, 2, 2, 2], F32)
        z_t = {}

        x_t = {}
        xh = {}
        x_rep = {}
        wide = {}
        z_bf = {}
        z_mx = {}
        w_grouped = {}
        w_permuted = {}
        b_grouped = {}
        y_grouped = {}
        y_rows = {}
        closed = []
        y_mx = {}
        acc = {}
        done = {0: 0, 1: 0}
        now = [0]
        owed = [0]

        def pay(columns):
            owed[0] = owed[0] - columns
        finished = {}

        def on_gpsimd(s):
            return s % ROUND == ROUND - 1

        def passes_of(r):
            return [s for s in range(r * ROUND, (r + 1) * ROUND) if 0 <= s < WIDE_PASSES]

        def gpsimd_first(passes):
            return [s for s in passes if on_gpsimd(s)] + [s for s in passes if not on_gpsimd(s)]

        def where(s):
            tile_no, gl = divmod(s, TILE_PASSES)
            it, b = divmod(tile_no, B)
            return b, it, gl

        def transpose_x(b, it, pool_name):
            xT_ps = tr_psum.tile([P, N_CHUNKS, P], BF16, tag="tr")
            for c in range(N_CHUNKS):
                nc.tensor.transpose(xT_ps[:, c, :], x_sb[(b, it)][:, c * P : (c + 1) * P], ident_bf[:])
            xT_sb = work.tile([P, N_CHUNKS, P], BF16, name=pool_name, bufs=1 if pool_name == "xT_turned" else 2)
            nc.scalar.copy(out=xT_sb[:], in_=xT_ps[:])
            x_t[(b, it)] = xT_sb

        def starts_tile(r):
            return len(passes_of(r)) > 0 and where(r * ROUND)[2] == 0

        def prepare(r):
            if starts_tile(r):
                b, it, gl = where(r * ROUND)
                transpose_x(b, it, "xT_sb")
                pay(M)

        def project_half(half):
            if half == 0:
                xh_ps = xh_psum.tile([P, M_CHUNKS, TILE_PASSES, CH_PASS], F32)
                xh[(0, 0)] = xh_ps
            for kc in range(M_CHUNKS):
                for c in range(N_CHUNKS):
                    nc.tensor.matmul(
                        xh[(0, 0)][:, kc, half * ROUND : (half + 1) * ROUND, :].rearrange("p g i -> p (g i)"),
                        lhsT=wb_sb[0][:, c, kc * P : (kc + 1) * P],
                        rhs=x_t[(0, 0)][:, c, half * ROUND * CH_PASS : (half + 1) * ROUND * CH_PASS],
                        start=(c == 0),
                        stop=(c == N_CHUNKS - 1),
                    )

        def project(r, chunks):
            if not starts_tile(r):
                return
            b, it, gl = where(r * ROUND)
            if chunks[0] == 0:
                xh_ps = xh_psum.tile([P, M_CHUNKS, TILE_PASSES, CH_PASS], F32)
                xh[(b, it)] = xh_ps
            for kc in chunks:
                for c in range(N_CHUNKS):
                    nc.tensor.matmul(
                        xh[(b, it)][:, kc, :, :].rearrange("p g i -> p (g i)"),
                        lhsT=wb_sb[b][:, c, kc * P : (kc + 1) * P],
                        rhs=x_t[(b, it)][:, c, :],
                        start=(c == 0),
                        stop=(c == N_CHUNKS - 1),
                    )

        def replicate(r):
            for s in gpsimd_first(passes_of(r)) if r > 0 else first_order:
                b, it, gl = where(s)
                rep_tile = wide_pool.tile([P, M_CHUNKS, CH_PASS, REP], F32, name="x_rep")
                nc.scalar.copy(
                    out=rep_tile[:],
                    in_=xh[(b, it)][:, :, gl, :]
                    .unsqueeze(3)
                    .to_broadcast([P, M_CHUNKS, CH_PASS, REP]),
                )
                x_rep[s] = rep_tile

        def widen(s):
            x_wide = wide_psum.tile([P, M], F32)
            for kc in range(M_CHUNKS):
                nc.tensor.transpose(
                    x_wide[:, kc * P : (kc + 1) * P],
                    x_rep[s][:, kc, :, :].rearrange("p i r -> p (i r)"),
                    ident_f32[:],
                )
            wide[s] = x_wide
            if on_gpsimd(s):
                x_wide_sb = wide_pool.tile([P, M], F32, bufs=2)
                nc.scalar.copy(out=x_wide_sb[:], in_=x_wide[:])
                wide[s] = x_wide_sb

        def multiply(s):
            if on_gpsimd(s):
                z_tile = z_pool.tile([P, M, PACK], BF16, align_bytes=64, name="z_gpsimd", bufs=1)
                engine = nc.gpsimd
            else:
                z_tile = z_pool.tile([P, M, PACK], BF16, align_bytes=64, name="z_vector", bufs=ROUND - 1)
                engine = nc.vector
            engine.tensor_tensor(
                out=z_tile[:],
                in0=wide[s][:].unsqueeze(2).to_broadcast([P, M, PACK]),
                in1=d_grouped[:],
                op=MULT,
            )
            z_bf[s] = z_tile

        def quantise(s):
            turned = s not in wide
            z_codes = z_pool.tile([P, M], U32, align_bytes=64, name="zt_codes" if turned else "z_codes", bufs=3 if turned else 2 * ROUND + 1)
            z_scales = z_pool.tile([P, M], U8, align_bytes=64, name="zt_scales" if turned else "z_scales", bufs=3 if turned else 2 * ROUND + 1)
            nc.vector.quantize_mx(
                out=z_codes[:].bitcast(FP8X4),
                scales=z_scales[:],
                in_=z_bf[s][:].rearrange("p b a k t -> p (b a k t)") if turned else z_bf[s][:].rearrange("p k t -> p (k t)"),
            )
            z_mx[s] = (z_codes, z_scales)

        def contract(s, b, g, r):
            if done[b] == 0:
                acc_tile = acc_psum.tile([P, M], F32, name="acc%d" % b)
                acc[b] = acc_tile
            z_codes, z_scales = z_mx[s]
            nc.tensor.matmul_mx(
                out=acc[b][:],
                lhsT=w_codes[:, g, :].bitcast(FP8X4),
                lhsT_scale=w_scales[:, g, :],
                rhs=z_codes[:].bitcast(FP8X4),
                rhs_scale=z_scales[:],
                start=(done[b] == 0),
                stop=(done[b] == WIDE_TILES * TILE_PASSES - 1),
            )
            done[b] = done[b] + 1
            if done[b] == WIDE_TILES * TILE_PASSES:
                closed.append(b)
                finished[b] = r

        def regroup_weights(h):
            words = (
                w_sb[h][:]
                .rearrange("o i j -> o (i j)")
                .bitcast(F32)
                .rearrange("o (g p u) -> o g p u", g=W_PASSES, p=P, u=2)
            )
            grouped = work.tile([P, W_PASSES, CO, PACK], BF16, align_bytes=64, name="w_grouped")
            for half in range(W_PASSES // 2):
                wT_ps = tr_psum.tile([P, 2, 2, CO], F32, tag="tr")
                for gg in range(2):
                    for u in range(2):
                        nc.tensor.transpose(
                            wT_ps[:, gg, u, :], words[:, 2 * half + gg, :, u], ident_f32[:]
                        )
                nc.scalar.copy(
                    out=grouped[:, 2 * half : 2 * half + 2, :, :].bitcast(F32),
                    in_=wT_ps[:].rearrange("p g u o -> p g o u"),
                )
            w_grouped[h] = grouped

        def quantise_weights(h):
            passes = slice(h * W_PASSES, (h + 1) * W_PASSES)
            nc.vector.quantize_mx(
                out=w_codes[:, passes, :].rearrange("p g o -> p (g o)").bitcast(FP8X4),
                scales=w_scales[:, passes, :].rearrange("p g o -> p (g o)"),
                in_=w_grouped[h][:].rearrange("p g o t -> p (g o t)"),
            )

        def regroup_bases(b, half):
            grouped = work.tile([P, N_CHUNKS // 2, P, PACK], BF16, align_bytes=64, name="b_grouped")
            for pp in range(2):
                words = bases_sb[(b, 2 * half + pp)][:].bitcast(F32).rearrange("n c (p u) -> n c p u", u=2)
                bT_ps = tr_psum.tile([P, 2, 2, P], F32, tag="tr")
                for cc in range(2):
                    for u in range(2):
                        nc.tensor.transpose(bT_ps[:, cc, u, :], words[:, cc, :, u], ident_f32[:])
                nc.scalar.copy(
                    out=grouped[:, 2 * pp : 2 * pp + 2, :, :].bitcast(F32),
                    in_=bT_ps[:].rearrange("p c u n -> p c n u"),
                )
            b_grouped[(b, half)] = grouped

        def quantise_bases(b, half):
            cols = slice(half * N_HALF, (half + 1) * N_HALF)
            nc.vector.quantize_mx(
                out=b_codes[b][:, cols].bitcast(FP8X4),
                scales=b_scales[b][:, cols],
                in_=b_grouped[(b, half)][:].rearrange("p c n t -> p (c n t)"),
            )

        def vector_is_free():
            return not passes_of(now[0])

        def fetch_y_hat(b):
            y_sb = work.tile([P, M], F32, name="f32_row", bufs=4)
            if vector_is_free() and b == 1:
                nc.vector.tensor_copy(out=y_sb[:], in_=acc[b][:])
            else:
                nc.scalar.copy(out=y_sb[:], in_=acc[b][:])
            y_rows[b] = y_sb

        def regroup_y_hat(b):
            y_cols = y_rows[b][:].rearrange("o (p t) -> o t p", t=PACK)
            yT_ps = tr_psum.tile([P, PACK, CO], F32, tag="tr")
            for t in range(PACK):
                nc.tensor.transpose(yT_ps[:, t, :], y_cols[:, t, :], ident_f32[:])
            grouped = work.tile([P, CO, PACK], BF16, align_bytes=64, name="y_grouped")
            if vector_is_free() and b == 1:
                nc.vector.tensor_copy(out=grouped[:], in_=yT_ps[:].rearrange("p t o -> p o t"))
            else:
                nc.scalar.copy(out=grouped[:], in_=yT_ps[:].rearrange("p t o -> p o t"))
            y_grouped[b] = grouped

        def quantise_y_hat(b):
            y_codes = work.tile([P, CO], U32, align_bytes=64)
            y_scales = work.tile([P, CO], U8, align_bytes=64)
            nc.vector.quantize_mx(
                out=y_codes[:].bitcast(FP8X4),
                scales=y_scales[:],
                in_=y_grouped[b][:].rearrange("p o t -> p (o t)"),
            )
            y_mx[b] = (y_codes, y_scales)

        def reconstruct(b):
            y_codes, y_scales = y_mx[b]
            for half in range(N // N_HALF):
                cols = slice(half * N_HALF, (half + 1) * N_HALF)
                o_ps = tr_psum.tile([P, N_HALF], F32, tag="tr")
                nc.tensor.matmul_mx(
                    out=o_ps[:],
                    lhsT=y_codes[:].bitcast(FP8X4),
                    lhsT_scale=y_scales[:],
                    rhs=b_codes[b][:, cols].bitcast(FP8X4),
                    rhs_scale=b_scales[b][:, cols],
                    start=True,
                    stop=True,
                )
                o_sb = work.tile([P, N_HALF], F32, name="f32_row", bufs=4)
                if half == 0 or not vector_is_free():
                    nc.scalar.copy(out=o_sb[:], in_=o_ps[:])
                else:
                    nc.vector.tensor_copy(out=o_sb[:], in_=o_ps[:])
                nc.sync.dma_start(out=out[b, :, cols], in_=o_sb[:])

        def transpose_d(halves):
            for half in halves:
                dT_ps = tr_psum.tile([P, 2, PACK, P], BF16, tag="tr")
                for cc in range(2):
                    kc = 2 * half + cc
                    for t in range(PACK):
                        nc.tensor.transpose(dT_ps[:, cc, t, :], d_rows[:, t, kc * P : (kc + 1) * P], ident_bf[:])
                nc.scalar.copy(
                    out=d_t[:, 2 * half : 2 * half + 2, :].rearrange("k c (p t) -> k c p t", t=PACK),
                    in_=dT_ps[:, :, :, 0:REP].rearrange("k c t p -> k c p t"),
                )

        def project_turned(b, chunks):
            if chunks[0] == 0:
                xh_ps = tr_psum.tile([P, M_CHUNKS, P], F32, tag="tr")
                xh[(b, TURNED_TILE)] = xh_ps
            xh_ps = xh[(b, TURNED_TILE)]
            for kc in chunks:
                for c in range(N_CHUNKS):
                    nc.tensor.matmul(
                        xh_ps[:, kc, :],
                        lhsT=wb_sb[b][:, c, kc * P : (kc + 1) * P],
                        rhs=x_t[(b, TURNED_TILE)][:, c, :],
                        start=(c == 0),
                        stop=(c == N_CHUNKS - 1),
                    )
            if chunks[-1] != M_CHUNKS - 1:
                return
            source = xh_ps[:].rearrange("k c (y a m e r) -> k (c y) a m r e", y=PAIRS, a=2, m=2, e=2)
            for a in range(2):
                for m in range(2):
                    nc.scalar.copy(out=xh_t[:, :, b, :, m, a, :], in_=source[:, :, a, m, :, :])

        def multiply_turned(on_scalar, b, kc, j):
            if kc not in z_t:
                z_tile = keep.tile([P, 2, PAIRS, B, CLASSES, KM // 2, LINE], BF16, name="z_t", bufs=2)
                z_t[kc] = z_tile
            pairs = slice(kc * PAIRS, (kc + 1) * PAIRS)
            if b is None:
                product = z_t[kc][:, j % 2, :, :, :, j // 2, :].rearrange("k y b r l -> k (y b r) l")
                factor = xh_t[:, pairs, :, :, :, :, :].rearrange("k y b r m a e -> k (y b r) (m a e)")
            else:
                product = z_t[kc][:, j % 2, :, b, :, j // 2, :]
                factor = xh_t[:, pairs, b, :, :, :, :].rearrange("k y r m a e -> k y r (m a e)")
            if on_scalar:
                nc.scalar.activation(
                    out=product,
                    in_=factor,
                    func=COPY,
                    scale=d_t[:, kc, j : j + 1],
                )
            else:
                nc.gpsimd.tensor_scalar(
                    out=product,
                    in0=factor,
                    scalar1=d_t[:, kc, j : j + 1],
                    scalar2=0.0,
                    op0=MULT,
                    op1=ADD,
                )

        def turn(kc, y):
            z_tile = z_pool.tile([P, B, 2, P, PACK], BF16, align_bytes=64, name="z_turned", bufs=3)
            words = (
                z_t[kc][:]
                .rearrange("k u y b r q l -> k (u y b r q l)")
                .bitcast(F32)
                .rearrange("k (u y b w) -> k u y b w", u=2, y=PAIRS, b=B)
            )
            for b in range(B):
                zT_ps = tr_psum.tile([P, 2, 2, P], F32, tag="tr")
                for u in range(2):
                    for a in range(2):
                        nc.tensor.transpose(zT_ps[:, u, a, :], words[:, u, y, b, a : 2 * P : 2], ident_f32[:])
                nc.scalar.copy(
                    out=z_tile[:, b, :, :, :].bitcast(F32),
                    in_=zT_ps[:].rearrange("p u a k -> p a k u"),
                )
            z_bf[(kc, y)] = z_tile

        def contract_turned(kc, y):
            z_codes, z_scales = z_mx[(kc, y)]
            for b in range(B):
                for a in range(2):
                    g = TURNED_TILE * TILE_PASSES + 2 * y + a
                    cols = slice((2 * b + a) * P, (2 * b + a + 1) * P)
                    nc.tensor.matmul_mx(
                        out=acc[b][:, kc * P : (kc + 1) * P],
                        lhsT=w_codes[:, g, :].bitcast(FP8X4),
                        lhsT_scale=w_scales[:, g, :],
                        rhs=z_codes[:, cols].bitcast(FP8X4),
                        rhs_scale=z_scales[:, cols],
                        start=False,
                        stop=False,
                    )

        def permute_weights_turned(h):
            source = w_sb[h][:].rearrange("o i j -> o (i j)").rearrange(
                "o (g m e q u) -> o g u e q m", g=W_PASSES, m=2, e=2, u=2
            )
            w_perm = work.tile([P, W_PASSES, 2, 2, P // 2, 2], BF16, align_bytes=64, name="b_grouped")
            for g in range(W_PASSES):
                for u in range(2):
                    nc.scalar.copy(out=w_perm[:, g, u, :, :, :], in_=source[:, g, u, :, :, :])
            w_permuted[h] = w_perm
            load_next_weights()

        def regroup_weights_turned(h):
            w_perm = w_permuted[h]
            grouped = work.tile([P, W_PASSES, CO, PACK], BF16, align_bytes=64, name="w_grouped")
            for half in range(W_PASSES // 2):
                wT_ps = tr_psum.tile([P, 2, PACK, CO], BF16, tag="tr")
                for gg in range(2):
                    for t in range(PACK):
                        nc.tensor.transpose(
                            wT_ps[:, gg, t, :],
                            w_perm[:, 2 * half + gg, t // 2, t % 2, :, :].rearrange("o q m -> o (q m)"),
                            ident_bf[:],
                        )
                nc.scalar.copy(
                    out=grouped[:, 2 * half : 2 * half + 2, :, :],
                    in_=wT_ps[:].rearrange("p g t o -> p g o t"),
                )
            w_grouped[h] = grouped

        for_vector = {}
        weights_round = [0]

        def later(r, job):
            for_vector.setdefault(r, []).append(job)

        def regroup_for(passes):
            for s in passes:
                b, it, gl = where(s)
                if b == 0 and gl % W_PASSES == 0:
                    regroup_weights((it * TILE_PASSES + gl) // W_PASSES)
                    pay(2 * M)
                    load_next_weights()

        def quantise_for(passes):
            for s in passes:
                b, it, gl = where(s)
                if b == 0 and gl % W_PASSES == 0:
                    quantise_weights((it * TILE_PASSES + gl) // W_PASSES)

        def turned_weights(h, r):
            regroup_weights_turned(h)
            later(r + 1, lambda: quantise_weights(h))
            weights_round[0] = r

        def turned_bases(b, half, r):
            regroup_bases(b, half)
            later(r + 1, lambda: quantise_bases(b, half))

        all_chunks = list(range(M_CHUNKS))
        first_order = [0, ROUND - 1] + list(range(1, ROUND - 1))
        prepare(0)
        project_half(0)
        replicate(0)
        for s in first_order:
            widen(s)
        project_half(1)
        replicate(1)

        for_gpsimd = []
        turned_ready = []

        def job_multiply(b, kc, j):
            def run():
                if j == 0 and b != 0:
                    for jj in range(KM - ON_GPSIMD, KM):
                        for_gpsimd.append((kc, jj))
                multiply_turned(True, b, kc, j)
            return run

        def job_turn(kc, y):
            def run():
                turn(kc, y)
                turned_ready.append((kc, y))
            return run

        products = {}
        for kc in range(M_CHUNKS):
            products[kc] = []
            for b in range(B) if kc == 0 else [None]:
                for j in range(KM - ON_GPSIMD):
                    products[kc].append((P if kc == 0 else 2 * P, job_multiply(b, kc, j), 2 if b == 1 else 0))
                    if b == 1 and j in (2, 8, 14, 20):
                        h = 6 + j // 12
                        if j % 12 == 2:
                            products[kc].append((4 * M, lambda h=h: permute_weights_turned(h), 0))
                        else:
                            products[kc].append((4 * M, lambda h=h: turned_weights(h, now[0]), 0))
        products[M_CHUNKS] = []
        chain = list(products[0])
        for kc in range(M_CHUNKS):
            count = len(products[kc + 1])
            for y in range(PAIRS):
                chain.append((2 * M, job_turn(kc, y), -1 - kc))
                chain.extend(products[kc + 1][y * count // PAIRS : (y + 1) * count // PAIRS])
                if kc in (1, 2) and y % 2 == 1:
                    chain.append((2 * M, lambda b=kc - 1, half=y // 2: turned_bases(b, half, now[0]), 0))
        at = [0]

        def turned_work(columns):
            owed[0] = owed[0] + columns
            turned = 0
            while at[0] < len(chain) and owed[0] > 0:
                cost, job, kind = chain[at[0]]
                is_pass = kind < 0
                if is_pass and (turned == 1 or any(kc <= -1 - kind for kc, j in for_gpsimd)):
                    return
                if is_pass and now[0] <= weights_round[0]:
                    return
                if not is_pass and kind > now[0]:
                    return
                turned = turned + (1 if is_pass else 0)
                at[0] = at[0] + 1
                owed[0] = owed[0] - cost
                job()

        rounds = WIDE_PASSES // ROUND
        fresh = []
        at_end = []
        held = []
        turned_left = [M_CHUNKS * PAIRS]
        for r in range(rounds + 5):
            now[0] = r
            nxt = gpsimd_first(passes_of(r + 1))
            held.extend(passes_of(r - 1) if r > 2 else passes_of(0) + passes_of(1) if r == 2 else [])
            last = []
            for s in held:
                b, it, gl = where(s)
                if on_gpsimd(s):
                    last.append(s)
                else:
                    contract(s, b, it * TILE_PASSES + gl, r)
            held.clear()
            for key in fresh:
                contract_turned(key[0], key[1])
                turned_left[0] = turned_left[0] - 1
            fresh.clear()
            for s in last:
                b, it, gl = where(s)
                if it == WIDE_TILES - 1 and gl == TILE_PASSES - 1 and turned_left[0] > 0:
                    held.append(s)
                else:
                    contract(s, b, it * TILE_PASSES + gl, r)
            for b in closed:
                fetch_y_hat(b)
            for b in closed:
                regroup_y_hat(b)
            closed.clear()
            for b in range(B):
                if finished.get(b) == r - 1:
                    reconstruct(b)
            prepare(r + 2)
            if r == 1:
                transpose_x(1, TURNED_TILE, "xT_turned")
                pay(M)
            if r == 5:
                for pair in range(4):
                    load_bases(1, pair)
            for n in range(ROUND):
                if r == 0 and n == 0:
                    transpose_x(0, TURNED_TILE, "xT_turned")
                if n < len(nxt):
                    widen(nxt[n])
                if r > 0:
                    project(r + 2, [n])
                if r == 0 and n < 2:
                    project(2, [2 * n, 2 * n + 1])
                if r == 0 and n == 1:
                    replicate(2)
                if r == 0 and n == 2:
                    transpose_d([0, 1])
                if r == 0 and n == 3:
                    project_turned(0, all_chunks)
                if r == 1:
                    project_turned(1, [n])
                    pay(P)
                if r > 0:
                    turned_work(SLOT_COLUMNS)
                if n == ROUND - 3:
                    at_end.extend(turned_ready)
                    turned_ready.clear()
            if r == 0:
                load_bases(0, 2)
                load_bases(0, 3)
                regroup_for(passes_of(0) + passes_of(1))
                turned_work(2 * SLOT_COLUMNS)
            if r > 0:
                replicate(r + 2)
                regroup_for(passes_of(r + 1))
            for s in gpsimd_first(passes_of(r)) if r > 0 else first_order:
                multiply(s)
                if on_gpsimd(s):
                    for kc, j in for_gpsimd[0:GPSIMD_A_ROUND]:
                        multiply_turned(False, None, kc, j)
                    rest = for_gpsimd[GPSIMD_A_ROUND:]
                    for_gpsimd.clear()
                    for_gpsimd.extend(rest)
            if not passes_of(r):
                for kc, j in for_gpsimd:
                    multiply_turned(False, None, kc, j)
                for_gpsimd.clear()
            for job in for_vector.get(r, []):
                job()
            for b in range(B):
                if finished.get(b) == r:
                    quantise_y_hat(b)
            for s in passes_of(r):
                if not on_gpsimd(s):
                    quantise(s)
            quantise_for(passes_of(r) if r > 1 else passes_of(0) + passes_of(1) if r == 1 else [])
            for key in at_end:
                quantise(key)
            fresh.extend(at_end)
            at_end.clear()
            for s in passes_of(r):
                if on_gpsimd(s):
                    quantise(s)
        assert at[0] == len(chain) and not held and not for_gpsimd and len(y_mx) == B
